import numpy as np
import ml_dtypes


def mxq(x, axis, fmt="e4m3"):
    dtype, down = {"e4m3": (ml_dtypes.float8_e4m3fn, 7), "e5m2": (ml_dtypes.float8_e5m2, 14)}[fmt]
    v = np.moveaxis(np.asarray(x, np.float32).astype(ml_dtypes.bfloat16).astype(np.float64), axis, -1)
    blocks = v.reshape(v.shape[:-1] + (-1, 32))
    amax = np.abs(blocks).max(-1, keepdims=True)
    byte = np.maximum(np.where(amax > 0, np.frexp(amax)[1] - 1 + 127, 0) - down, 1)
    scale = np.exp2(byte - 127.0)
    codes = (blocks / scale).astype(np.float32).astype(dtype).astype(np.float64)
    return np.moveaxis((codes * scale).reshape(v.shape), -1, axis)


WIDE = False


def mx_kscale(k):
    if not WIDE:
        return np.ones(k)
    levels = np.array([10, -10, 5, -5, 0])
    if k % 512:
        return np.exp2(np.random.permutation(np.resize(levels, k // 32))).repeat(32)
    a = np.empty((k // 512, 16))
    for p in range(k // 512):
        a[p, :8] = np.random.permutation(np.resize(levels, 8))
        for g in range(8):
            far = levels[np.abs(levels - a[p, g]) >= 10]
            a[p, g + 8] = far[np.random.randint(len(far))]
    return np.exp2(a.ravel()).repeat(32)


BF16 = ml_dtypes.bfloat16


def bf(x):
    return np.asarray(x, np.float32).astype(BF16)


def f64(x):
    return np.asarray(x).astype(np.float64)


S, D, H, DH, F = 8192, 1024, 1, 128, 4096
E = H * DH
EPS = 1e-5
XS = 0.015


def fixed_pos_embedding(seq_len, dim):
    inv_freq = 1.0 / (10000.0 ** (np.arange(0, dim, 2) / dim))
    sinusoid = np.arange(seq_len, dtype=np.float64)[:, None] * inv_freq[None, :]
    sin = np.concatenate([np.sin(sinusoid)] * 2, axis=-1)[:, :dim]
    cos = np.concatenate([np.cos(sinusoid)] * 2, axis=-1)[:, :dim]
    return sin, cos


def rotate_every_two(y):
    return np.stack((-y[..., 1::2], y[..., ::2]), axis=-1).reshape(y.shape)


def apply_rotary(y, sin, cos):
    return rotate_every_two(y) * sin[:, None, :] + y * cos[:, None, :]


def layernorm(x, scale, offset):
    mean = x.mean(axis=-1, keepdims=True)
    var = x.var(axis=-1, keepdims=True)
    return scale / np.sqrt(var + EPS) * (x - mean) + offset


def setup_inputs():
    s = mx_kscale(D)
    x = np.random.standard_normal((S, D)) + 0.5 * np.random.standard_normal(S)[:, None]
    return {"x": bf(XS * x[None]),
            "ln_scale": bf((1.0 + 0.1 * np.random.standard_normal(D)) * s),
            "ln_offset": bf(0.1 * np.random.standard_normal(D) * s),
            "Wq": bf(np.random.standard_normal((D, E)) * 0.7 / np.sqrt(D) / s[:, None]),
            "Wk": bf(np.random.standard_normal((D, E)) * 0.7 / np.sqrt(D) / s[:, None]),
            "Wv": bf(np.random.standard_normal((D, E)) / np.sqrt(D) / s[:, None])}


def reference(x, ln_scale, ln_offset, Wq, Wk, Wv):
    x = f64(x)
    b, s, _ = x.shape
    xn = layernorm(x, f64(ln_scale), f64(ln_offset))
    xq = mxq(xn, 2, "e4m3")

    def proj(W):
        h = (xq @ mxq(f64(W), 0, "e4m3")).reshape(b, s, H, DH)
        return np.transpose(h, (1, 0, 2, 3)).reshape(s, b * H, DH)

    q, v, k = proj(Wq), proj(Wv), proj(Wk)
    sin, cos = fixed_pos_embedding(s, DH)
    return apply_rotary(q, sin, cos), apply_rotary(k, sin, cos), v

@@ -1,0 +1,422 @@
+import math
+from contextlib import ExitStack
+
+import concourse.mybir as mybir
+from concourse.masks import make_identity
+
+F32 = mybir.dt.float32
+BF16 = mybir.dt.bfloat16
+I32 = mybir.dt.int32
+U32 = mybir.dt.uint32
+U8 = mybir.dt.uint8
+FP8X4 = mybir.dt.float8_e4m3fn_x4
+ALU = mybir.AluOpType
+ACT = mybir.ActivationFunctionType
+
+P = 128
+S = 8192
+D = 1024
+DH = 128
+EPS = 1e-5
+PACK = 4
+CHUNKS = D // P
+PASSES = D // (P * PACK)
+TILES = S // P
+GROUP = 2
+GROUPS = TILES // GROUP
+BANK = 512
+ROWS = GROUP * P
+PSUM_BANKS = 8
+FREQS = DH // 2
+ROUND_MAGIC = 12582912.0
+HI_GRID = 2.0 ** 19
+TABLE_STEP = 16
+LOADS_AHEAD = 4
+
+FLOPS = 2 * S * D * 3 * DH
+
+
+def load_layer_norm_columns(nc, setup, keep, banks, ident, ln_scale, ln_offset):
+    rows = setup.tile([P, BANK], BF16, name="gb_rows")
+    nc.vector.memset(rows[:], 0.0)
+    nc.sync.dma_start(out=rows[0:PASSES, :], in_=ln_scale.rearrange("(h k) -> h k", h=PASSES))
+    nc.sync.dma_start(
+        out=rows[PASSES : 2 * PASSES, :], in_=ln_offset.rearrange("(h k) -> h k", h=PASSES)
+    )
+    rows32 = setup.tile([P, PACK, P], F32, name="gb_rows32")
+    nc.vector.tensor_copy(out=rows32[:], in_=rows[:].rearrange("r (p j) -> r j p", j=PACK))
+    turned = banks.tile([P, PACK, P], F32, tag="turned")
+    for j in range(PACK):
+        nc.tensor.transpose(turned[:, j, :], rows32[:, j, :], ident[:])
+    gain_bias = keep.tile([P, 2 * CHUNKS], F32, name="gain_bias")
+    nc.vector.tensor_copy(
+        out=gain_bias[:].rearrange("p (g j) -> p g j", j=PACK),
+        in_=turned[:, :, 0 : 2 * PASSES].rearrange("p j g -> p g j"),
+    )
+    return gain_bias
+
+
+def quantise_weights(nc, setup, keep, Wq, Wk, Wv):
+    qk_grouped = setup.tile([P, PASSES, BANK, PACK], BF16, name="qk_grouped", align_bytes=64)
+    v_grouped = setup.tile([P, PASSES, DH, PACK], BF16, name="v_grouped", align_bytes=64)
+    for g, w in enumerate((Wq, Wk)):
+        raw = setup.tile([P, CHUNKS, DH], BF16, name="w_raw%d" % g)
+        nc.sync.dma_start(
+            out=raw[:].rearrange("p (h j) n -> p h j n", j=PACK),
+            in_=w.rearrange("(h p j) n -> p h j n", p=P, j=PACK),
+        )
+        for h in range(PASSES):
+            rows = raw[:, h * PACK : (h + 1) * PACK, :]
+            cols = qk_grouped[:, h, g * 2 * DH : (g + 1) * 2 * DH, :]
+            nc.vector.tensor_copy(
+                out=cols.rearrange("p (r s c) j -> p r s c j", r=2, s=2)[:, :, 0, :, :],
+                in_=rows.rearrange("p j (r c) -> p r c j", r=2),
+            )
+            for e in range(2):
+                nc.vector.tensor_copy(
+                    out=cols.rearrange("p (r s i e) j -> p r s i e j", r=2, s=2, e=2)[
+                        :, :, 1, :, e, :
+                    ],
+                    in_=rows.rearrange("p j (r i e) -> p r i e j", r=2, e=2)[:, :, :, 1 - e, :],
+                )
+    raw = setup.tile([P, CHUNKS, DH], BF16, name="w_raw2")
+    nc.sync.dma_start(
+        out=raw[:].rearrange("p (h j) n -> p h j n", j=PACK),
+        in_=Wv.rearrange("(h p j) n -> p h j n", p=P, j=PACK),
+    )
+    for h in range(PASSES):
+        nc.vector.tensor_copy(
+            out=v_grouped[:, h, :, :],
+            in_=raw[:, h * PACK : (h + 1) * PACK, :].rearrange("p j n -> p n j"),
+        )
+
+    qk_codes = keep.tile([P, PASSES, BANK], U32, name="qk_codes", align_bytes=64)
+    qk_scales = keep.tile([P, PASSES, BANK], U8, name="qk_scales", align_bytes=64)
+    v_codes = keep.tile([P, PASSES, DH], U32, name="v_codes", align_bytes=64)
+    v_scales = keep.tile([P, PASSES, DH], U8, name="v_scales", align_bytes=64)
+    for h in range(PASSES):
+        nc.vector.quantize_mx(
+            out=qk_codes[:, h, :].bitcast(FP8X4),
+            scales=qk_scales[:, h, :],
+            in_=qk_grouped[:, h, :, :].rearrange("p c j -> p (c j)"),
+        )
+        nc.vector.quantize_mx(
+            out=v_codes[:, h, :].bitcast(FP8X4),
+            scales=v_scales[:, h, :],
+            in_=v_grouped[:, h, :, :].rearrange("p c j -> p (c j)"),
+        )
+    return qk_codes, qk_scales, v_codes, v_scales
+
+
+def turns_per_position(c):
+    sign = -1.0 if c % 2 == 0 else 1.0
+    turns = sign * 10000.0 ** (-c / FREQS) / (2.0 * math.pi)
+    coarse = round(turns * HI_GRID) / HI_GRID
+    return coarse, turns - coarse
+
+
+def fine_frequencies(nc, setup, one):
+    turns_lo = setup.tile([P, FREQS], F32, name="turns_lo")
+    for c in range(FREQS):
+        nc.vector.tensor_scalar(
+            out=turns_lo[:, c : c + 1], in0=one[:], scalar1=turns_per_position(c)[1],
+            scalar2=None, op0=ALU.mult,
+        )
+    return turns_lo
+
+
+def coarse_frequencies(nc, setup):
+    turns_hi = setup.tile([P, FREQS], F32, name="turns_hi")
+    for c in range(FREQS):
+        nc.vector.memset(turns_hi[:, c : c + 1], turns_per_position(c)[0])
+    return turns_hi
+
+
+def first_angles(nc, setup, first_i, turns_hi, turns_lo):
+    first = setup.tile([P, 1], F32, name="first")
+    nc.vector.tensor_copy(out=first[:], in_=first_i[:])
+    coarse = setup.tile([P, FREQS], F32, name="coarse")
+    nc.vector.tensor_scalar(
+        out=coarse[:], in0=turns_hi[:], scalar1=first[:, 0:1], scalar2=None, op0=ALU.mult
+    )
+    whole = setup.tile([P, FREQS], F32, name="whole")
+    nc.vector.tensor_scalar(
+        out=whole[:], in0=coarse[:], scalar1=ROUND_MAGIC, scalar2=ROUND_MAGIC,
+        op0=ALU.add, op1=ALU.subtract,
+    )
+    nc.vector.tensor_tensor(out=coarse[:], in0=coarse[:], in1=whole[:], op=ALU.subtract)
+    angle = setup.tile([P, TILES, FREQS], F32, name="angle")
+    nc.vector.scalar_tensor_tensor(
+        out=angle[:, 0, :], in0=turns_lo[:], scalar=first[:, 0:1], in1=coarse[:],
+        op0=ALU.mult, op1=ALU.add,
+    )
+    return angle
+
+
+def all_angles(nc, setup, angle, turns_hi, turns_lo):
+    turns_all = setup.tile([P, FREQS], F32, name="turns_all")
+    nc.vector.tensor_tensor(out=turns_all[:], in0=turns_hi[:], in1=turns_lo[:], op=ALU.add)
+    filled = 1
+    while filled < TILES:
+        nc.vector.scalar_tensor_tensor(
+            out=angle[:, filled : 2 * filled, :],
+            in0=turns_all[:].unsqueeze(1).to_broadcast([P, filled, FREQS]),
+            scalar=float(filled),
+            in1=angle[:, 0:filled, :],
+            op0=ALU.mult,
+            op1=ALU.add,
+        )
+        filled *= 2
+    for start in range(0, TILES, TABLE_STEP):
+        part = angle[:, start : start + TABLE_STEP, :]
+        whole_turns = setup.tile([P, TABLE_STEP, FREQS], F32, tag="whole_turns", bufs=2)
+        nc.vector.tensor_scalar(
+            out=whole_turns[:], in0=part, scalar1=ROUND_MAGIC, scalar2=ROUND_MAGIC,
+            op0=ALU.add, op1=ALU.subtract,
+        )
+        nc.gpsimd.tensor_tensor(out=part, in0=part, in1=whole_turns[:], op=ALU.subtract)
+
+
+def sines_and_cosines(nc, setup, keep, angle):
+    table = keep.tile([P, TILES, 2, FREQS], F32, name="table")
+    for start in range(0, TILES, TABLE_STEP):
+        part = angle[:, start : start + TABLE_STEP, :]
+        nc.scalar.activation(
+            out=table[:, start : start + TABLE_STEP, 1, :], in_=part, func=ACT.Sin,
+            scale=2.0 * math.pi,
+        )
+        half_sine = setup.tile([P, TABLE_STEP, FREQS], F32, tag="half_sine", bufs=2)
+        nc.scalar.activation(out=half_sine[:], in_=part, func=ACT.Sin, scale=math.pi)
+        nc.vector.tensor_tensor(out=half_sine[:], in0=half_sine[:], in1=half_sine[:], op=ALU.mult)
+        nc.gpsimd.tensor_scalar(
+            out=table[:, start : start + TABLE_STEP, 0, :], in0=half_sine[:],
+            scalar1=-2.0, scalar2=1.0, op0=ALU.mult, op1=ALU.add,
+        )
+    return table
+
+
+def tile_transformerlayershard_pa_t_kernel(
+    tc, x, ln_scale, ln_offset, Wq, Wk, Wv, out_0, out_1, out_2
+):
+    nc = tc.nc
+    x_rows = x.rearrange("b (p t) d -> p (b t) d", t=TILES)
+    q_rows = out_0.rearrange("(p t) h j -> p t (h j)", t=TILES)
+    k_rows = out_1.rearrange("(p t) h j -> p t (h j)", t=TILES)
+    v_rows = out_2.rearrange("(p t) h j -> p t (h j)", t=TILES)
+
+    with ExitStack() as ctx:
+        keep = ctx.enter_context(tc.tile_pool(name="keep", bufs=1))
+        setup = ctx.enter_context(tc.tile_pool(name="setup", bufs=1))
+        loads = ctx.enter_context(tc.tile_pool(name="loads", bufs=LOADS_AHEAD))
+        stats = ctx.enter_context(tc.tile_pool(name="stats", bufs=4))
+        work = ctx.enter_context(tc.tile_pool(name="work", bufs=2))
+        banks = ctx.enter_context(tc.psum_pool(name="banks", bufs=PSUM_BANKS - GROUP - 1))
+        qk_banks = ctx.enter_context(tc.psum_pool(name="qk_banks", bufs=GROUP))
+        v_banks = ctx.enter_context(tc.psum_pool(name="v_banks", bufs=1))
+        ctx.enter_context(tc.manual_schedule())
+
+        x_of, neg_mean_of, spread_of, y_of, planes_of = {}, {}, {}, {}, {}
+        codes_of, scales_of, qk_acc_of, v_acc_of, products_of = {}, {}, {}, {}, {}
+        shared = {}
+
+        def load(n):
+            x_g = loads.tile([P, GROUP, D], BF16, tag="x_g")
+            nc.sync.dma_start(out=x_g[:], in_=x_rows[:, n * GROUP : (n + 1) * GROUP, :])
+            x_of[n] = x_g
+
+        def row_sums(n):
+            sums = stats.tile([P, GROUP], F32, tag="sums")
+            for t in range(GROUP):
+                unread_v = work.tile([P, D], BF16, tag="unread_v")
+                nc.vector.tensor_scalar(
+                    out=unread_v[:], in0=x_of[n][:, t, :], scalar1=1.0, scalar2=None,
+                    op0=ALU.mult, op1=ALU.add, accum_out=sums[:, t : t + 1],
+                )
+            neg_mean = stats.tile([P, GROUP], F32, tag="neg_mean")
+            nc.vector.tensor_scalar(
+                out=neg_mean[:], in0=sums[:], scalar1=-1.0 / D, scalar2=None, op0=ALU.mult
+            )
+            neg_mean_of[n] = neg_mean
+
+        def row_spread(n):
+            squares = stats.tile([P, GROUP], F32, tag="squares")
+            for t in range(GROUP):
+                unread_s = work.tile([P, D], BF16, tag="unread_s")
+                nc.scalar.activation(
+                    out=unread_s[:], in_=x_of[n][:, t, :], func=ACT.Square,
+                    bias=neg_mean_of[n][:, t : t + 1], scale=1.0,
+                    accum_out=squares[:, t : t + 1],
+                )
+            spread = stats.tile([P, GROUP], F32, tag="spread")
+            nc.scalar.activation(
+                out=spread[:], in_=squares[:], func=ACT.Sqrt, scale=1.0 / D,
+                bias=shared["eps"][:, 0:1],
+            )
+            spread_of[n] = spread
+
+        def normalise(n):
+            rstd = stats.tile([P, GROUP], F32, tag="rstd")
+            nc.vector.reciprocal(out=rstd[:], in_=spread_of[n][:])
+            y_g = work.tile([P, GROUP, D], F32, tag="y_g")
+            for t in range(GROUP):
+                nc.gpsimd.tensor_scalar(
+                    out=y_g[:, t, :].rearrange("r (h j p) -> r h j p", h=PASSES, j=PACK),
+                    in0=x_of[n][:, t, :].rearrange("r (h p j) -> r h j p", p=P, j=PACK),
+                    scalar1=neg_mean_of[n][:, t : t + 1], scalar2=rstd[:, t : t + 1],
+                    op0=ALU.add, op1=ALU.mult,
+                )
+            y_of[n] = y_g
+
+        def turn(n):
+            gain_bias = shared["gain_bias"]
+            planes = work.tile([P, CHUNKS, ROWS], BF16, tag="planes")
+            for c in range(CHUNKS):
+                turned = banks.tile([P, ROWS], F32, tag="turned")
+                for t in range(GROUP):
+                    nc.tensor.transpose(
+                        turned[:, t * P : (t + 1) * P], y_of[n][:, t, c * P : (c + 1) * P],
+                        shared["ident"][:],
+                    )
+                nc.scalar.activation(
+                    out=planes[:, c, :], in_=turned[:], func=ACT.Identity,
+                    scale=gain_bias[:, c : c + 1], bias=gain_bias[:, CHUNKS + c : CHUNKS + c + 1],
+                )
+            planes_of[n] = planes
+
+        def pack(n):
+            grouped = work.tile([P, PASSES, ROWS, PACK], BF16, tag="grouped", bufs=1, align_bytes=64)
+            codes = work.tile([P, PASSES, ROWS], U32, tag="codes", align_bytes=64)
+            scales = work.tile([P, PASSES, ROWS], U8, tag="scales", align_bytes=64)
+            for h in range(PASSES):
+                nc.vector.tensor_copy(
+                    out=grouped[:, h, :, :].rearrange("p (w i) j -> p w j i", i=4),
+                    in_=planes_of[n][:, h * PACK : (h + 1) * PACK, :].rearrange(
+                        "p j (w i) -> p w j i", i=4
+                    ),
+                )
+            for h in range(PASSES):
+                nc.vector.quantize_mx(
+                    out=codes[:, h, :].bitcast(FP8X4),
+                    scales=scales[:, h, :],
+                    in_=grouped[:, h, :, :].rearrange("p w j -> p (w j)"),
+                )
+            codes_of[n] = codes
+            scales_of[n] = scales
+
+        def project_tile(n, t):
+            qk_codes, qk_scales, v_codes, v_scales = shared["weights"]
+            codes, scales = codes_of[n], scales_of[n]
+            rows = slice(t * P, (t + 1) * P)
+            if t == 0:
+                v_acc_of[n] = v_banks.tile([P, GROUP * DH], F32, tag="v_acc", name="v_acc")
+            qk_acc = qk_banks.tile([P, BANK], F32, tag="qk_acc")
+            for h in range(PASSES):
+                nc.tensor.matmul_mx(
+                    out=qk_acc[:],
+                    lhsT=codes[:, h, rows].bitcast(FP8X4),
+                    lhsT_scale=scales[:, h, rows],
+                    rhs=qk_codes[:, h, :].bitcast(FP8X4),
+                    rhs_scale=qk_scales[:, h, :],
+                    start=(h == 0),
+                    stop=(h == PASSES - 1),
+                )
+            for h in range(PASSES):
+                nc.tensor.matmul_mx(
+                    out=v_acc_of[n][:, rows],
+                    lhsT=codes[:, h, rows].bitcast(FP8X4),
+                    lhsT_scale=scales[:, h, rows],
+                    rhs=v_codes[:, h, :].bitcast(FP8X4),
+                    rhs_scale=v_scales[:, h, :],
+                    start=(h == 0),
+                    stop=(h == PASSES - 1),
+                )
+            qk_acc_of[(n, t)] = qk_acc
+
+        def rotate_tile(n, t):
+            if t == 0:
+                products_of[n] = work.tile(
+                    [P, GROUP, 4, DH], F32, tag="products", name="products", bufs=1
+                )
+            nc.vector.tensor_tensor(
+                out=products_of[n][:, t, :, :],
+                in0=qk_acc_of[(n, t)][:].rearrange("p (a w) -> p a w", a=4),
+                in1=shared["table"][:, n * GROUP + t, :, :]
+                .rearrange("p s c -> p (s c)")
+                .unsqueeze(1)
+                .to_broadcast([P, 4, DH]),
+                op=ALU.mult,
+            )
+
+        def store_qk(n):
+            tiles = slice(n * GROUP, (n + 1) * GROUP)
+            products = products_of[n]
+            qk_out = work.tile([P, GROUP, 2, DH], F32, tag="qk_out")
+            nc.vector.tensor_tensor(
+                out=qk_out[:].rearrange("p t g (r c) -> p (t g r) c", r=2),
+                in0=products[:, :, :, 0:FREQS].rearrange("p t a c -> p (t a) c"),
+                in1=products[:, :, :, FREQS:DH].rearrange("p t a c -> p (t a) c"),
+                op=ALU.add,
+            )
+            nc.sync.dma_start(out=q_rows[:, tiles, :], in_=qk_out[:, :, 0, :])
+            nc.sync.dma_start(out=k_rows[:, tiles, :], in_=qk_out[:, :, 1, :])
+
+        def store_v(n):
+            tiles = slice(n * GROUP, (n + 1) * GROUP)
+            v_out = work.tile([P, GROUP, DH], F32, tag="v_out")
+            nc.vector.tensor_copy(out=v_out[:].rearrange("p t j -> p (t j)"), in_=v_acc_of[n][:])
+            nc.sync.dma_start(out=v_rows[:, tiles, :], in_=v_out[:])
+
+        def live(n):
+            return 0 <= n < GROUPS
+
+        def one_round(i):
+            if live(i + 5) and i + 5 >= LOADS_AHEAD:
+                load(i + 5)
+            if live(i + 1):
+                turn(i + 1)
+            if live(i):
+                pack(i)
+            if live(i - 2):
+                store_qk(i - 2)
+            if live(i + 2):
+                normalise(i + 2)
+            if live(i - 1):
+                store_v(i - 1)
+            for t in range(GROUP):
+                if live(i - 1):
+                    rotate_tile(i - 1, t)
+                if live(i):
+                    project_tile(i, t)
+            if live(i + 3):
+                row_spread(i + 3)
+            if live(i + 4):
+                row_sums(i + 4)
+
+        for n in range(LOADS_AHEAD):
+            load(n)
+        ident = keep.tile([P, P], F32, name="ident")
+        make_identity(nc, ident[:])
+        shared["ident"] = ident
+        first_i = setup.tile([P, 1], I32, name="first_i")
+        nc.gpsimd.iota(first_i[:], pattern=[[0, 1]], base=0, channel_multiplier=TILES)
+        one = setup.tile([P, 1], F32, name="one")
+        nc.vector.memset(one[:], 1.0)
+        eps = keep.tile([P, 1], F32, name="eps")
+        nc.vector.tensor_scalar(out=eps[:], in0=one[:], scalar1=EPS, scalar2=None, op0=ALU.mult)
+        shared["eps"] = eps
+        turns_lo = fine_frequencies(nc, setup, one)
+        one_round(-4)
+        one_round(-3)
+        shared["gain_bias"] = load_layer_norm_columns(
+            nc, setup, keep, banks, ident, ln_scale, ln_offset
+        )
+        one_round(-2)
+        turns_hi = coarse_frequencies(nc, setup)
+        angle = first_angles(nc, setup, first_i, turns_hi, turns_lo)
+        one_round(-1)
+        all_angles(nc, setup, angle, turns_hi, turns_lo)
+        shared["weights"] = quantise_weights(nc, setup, keep, Wq, Wk, Wv)
+        one_round(0)
+        shared["table"] = sines_and_cosines(nc, setup, keep, angle)
+        for i in range(1, GROUPS + 2):
+            one_round(i)

@@ -19,93 +19,23 @@ D = 1024
 DH = 128
 EPS = 1e-5
 PACK = 4
-CHUNKS = D // P
 PASSES = D // (P * PACK)
+SLOTS = PASSES * PACK
 TILES = S // P
-GROUP = 2
-GROUPS = TILES // GROUP
+UNIT = 2
+UNITS = TILES // UNIT
 BANK = 512
-ROWS = GROUP * P
-PSUM_BANKS = 8
 FREQS = DH // 2
+DECADE = FREQS // 4
 ROUND_MAGIC = 12582912.0
 HI_GRID = 2.0 ** 19
-TABLE_STEP = 16
-LOADS_AHEAD = 4
+STEP = 4
+TINY = 2.0 ** -60
+HEAD_TILES = 4
+VECTOR_SUM_EVERY = 6
+X_BUFS = 8
 
 FLOPS = 2 * S * D * 3 * DH
-
-
-def load_layer_norm_columns(nc, setup, keep, banks, ident, ln_scale, ln_offset):
-    rows = setup.tile([P, BANK], BF16, name="gb_rows")
-    nc.vector.memset(rows[:], 0.0)
-    nc.sync.dma_start(out=rows[0:PASSES, :], in_=ln_scale.rearrange("(h k) -> h k", h=PASSES))
-    nc.sync.dma_start(
-        out=rows[PASSES : 2 * PASSES, :], in_=ln_offset.rearrange("(h k) -> h k", h=PASSES)
-    )
-    rows32 = setup.tile([P, PACK, P], F32, name="gb_rows32")
-    nc.vector.tensor_copy(out=rows32[:], in_=rows[:].rearrange("r (p j) -> r j p", j=PACK))
-    turned = banks.tile([P, PACK, P], F32, tag="turned")
-    for j in range(PACK):
-        nc.tensor.transpose(turned[:, j, :], rows32[:, j, :], ident[:])
-    gain_bias = keep.tile([P, 2 * CHUNKS], F32, name="gain_bias")
-    nc.vector.tensor_copy(
-        out=gain_bias[:].rearrange("p (g j) -> p g j", j=PACK),
-        in_=turned[:, :, 0 : 2 * PASSES].rearrange("p j g -> p g j"),
-    )
-    return gain_bias
-
-
-def quantise_weights(nc, setup, keep, Wq, Wk, Wv):
-    qk_grouped = setup.tile([P, PASSES, BANK, PACK], BF16, name="qk_grouped", align_bytes=64)
-    v_grouped = setup.tile([P, PASSES, DH, PACK], BF16, name="v_grouped", align_bytes=64)
-    for g, w in enumerate((Wq, Wk)):
-        raw = setup.tile([P, CHUNKS, DH], BF16, name="w_raw%d" % g)
-        nc.sync.dma_start(
-            out=raw[:].rearrange("p (h j) n -> p h j n", j=PACK),
-            in_=w.rearrange("(h p j) n -> p h j n", p=P, j=PACK),
-        )
-        for h in range(PASSES):
-            rows = raw[:, h * PACK : (h + 1) * PACK, :]
-            cols = qk_grouped[:, h, g * 2 * DH : (g + 1) * 2 * DH, :]
-            nc.vector.tensor_copy(
-                out=cols.rearrange("p (r s c) j -> p r s c j", r=2, s=2)[:, :, 0, :, :],
-                in_=rows.rearrange("p j (r c) -> p r c j", r=2),
-            )
-            for e in range(2):
-                nc.vector.tensor_copy(
-                    out=cols.rearrange("p (r s i e) j -> p r s i e j", r=2, s=2, e=2)[
-                        :, :, 1, :, e, :
-                    ],
-                    in_=rows.rearrange("p j (r i e) -> p r i e j", r=2, e=2)[:, :, :, 1 - e, :],
-                )
-    raw = setup.tile([P, CHUNKS, DH], BF16, name="w_raw2")
-    nc.sync.dma_start(
-        out=raw[:].rearrange("p (h j) n -> p h j n", j=PACK),
-        in_=Wv.rearrange("(h p j) n -> p h j n", p=P, j=PACK),
-    )
-    for h in range(PASSES):
-        nc.vector.tensor_copy(
-            out=v_grouped[:, h, :, :],
-            in_=raw[:, h * PACK : (h + 1) * PACK, :].rearrange("p j n -> p n j"),
-        )
-
-    qk_codes = keep.tile([P, PASSES, BANK], U32, name="qk_codes", align_bytes=64)
-    qk_scales = keep.tile([P, PASSES, BANK], U8, name="qk_scales", align_bytes=64)
-    v_codes = keep.tile([P, PASSES, DH], U32, name="v_codes", align_bytes=64)
-    v_scales = keep.tile([P, PASSES, DH], U8, name="v_scales", align_bytes=64)
-    for h in range(PASSES):
-        nc.vector.quantize_mx(
-            out=qk_codes[:, h, :].bitcast(FP8X4),
-            scales=qk_scales[:, h, :],
-            in_=qk_grouped[:, h, :, :].rearrange("p c j -> p (c j)"),
-        )
-        nc.vector.quantize_mx(
-            out=v_codes[:, h, :].bitcast(FP8X4),
-            scales=v_scales[:, h, :],
-            in_=v_grouped[:, h, :, :].rearrange("p c j -> p (c j)"),
-        )
-    return qk_codes, qk_scales, v_codes, v_scales
 
 
 def turns_per_position(c):
@@ -113,86 +43,6 @@ def turns_per_position(c):
     turns = sign * 10000.0 ** (-c / FREQS) / (2.0 * math.pi)
     coarse = round(turns * HI_GRID) / HI_GRID
     return coarse, turns - coarse
-
-
-def fine_frequencies(nc, setup, one):
-    turns_lo = setup.tile([P, FREQS], F32, name="turns_lo")
-    for c in range(FREQS):
-        nc.vector.tensor_scalar(
-            out=turns_lo[:, c : c + 1], in0=one[:], scalar1=turns_per_position(c)[1],
-            scalar2=None, op0=ALU.mult,
-        )
-    return turns_lo
-
-
-def coarse_frequencies(nc, setup):
-    turns_hi = setup.tile([P, FREQS], F32, name="turns_hi")
-    for c in range(FREQS):
-        nc.vector.memset(turns_hi[:, c : c + 1], turns_per_position(c)[0])
-    return turns_hi
-
-
-def first_angles(nc, setup, first_i, turns_hi, turns_lo):
-    first = setup.tile([P, 1], F32, name="first")
-    nc.vector.tensor_copy(out=first[:], in_=first_i[:])
-    coarse = setup.tile([P, FREQS], F32, name="coarse")
-    nc.vector.tensor_scalar(
-        out=coarse[:], in0=turns_hi[:], scalar1=first[:, 0:1], scalar2=None, op0=ALU.mult
-    )
-    whole = setup.tile([P, FREQS], F32, name="whole")
-    nc.vector.tensor_scalar(
-        out=whole[:], in0=coarse[:], scalar1=ROUND_MAGIC, scalar2=ROUND_MAGIC,
-        op0=ALU.add, op1=ALU.subtract,
-    )
-    nc.vector.tensor_tensor(out=coarse[:], in0=coarse[:], in1=whole[:], op=ALU.subtract)
-    angle = setup.tile([P, TILES, FREQS], F32, name="angle")
-    nc.vector.scalar_tensor_tensor(
-        out=angle[:, 0, :], in0=turns_lo[:], scalar=first[:, 0:1], in1=coarse[:],
-        op0=ALU.mult, op1=ALU.add,
-    )
-    return angle
-
-
-def all_angles(nc, setup, angle, turns_hi, turns_lo):
-    turns_all = setup.tile([P, FREQS], F32, name="turns_all")
-    nc.vector.tensor_tensor(out=turns_all[:], in0=turns_hi[:], in1=turns_lo[:], op=ALU.add)
-    filled = 1
-    while filled < TILES:
-        nc.vector.scalar_tensor_tensor(
-            out=angle[:, filled : 2 * filled, :],
-            in0=turns_all[:].unsqueeze(1).to_broadcast([P, filled, FREQS]),
-            scalar=float(filled),
-            in1=angle[:, 0:filled, :],
-            op0=ALU.mult,
-            op1=ALU.add,
-        )
-        filled *= 2
-    for start in range(0, TILES, TABLE_STEP):
-        part = angle[:, start : start + TABLE_STEP, :]
-        whole_turns = setup.tile([P, TABLE_STEP, FREQS], F32, tag="whole_turns", bufs=2)
-        nc.vector.tensor_scalar(
-            out=whole_turns[:], in0=part, scalar1=ROUND_MAGIC, scalar2=ROUND_MAGIC,
-            op0=ALU.add, op1=ALU.subtract,
-        )
-        nc.gpsimd.tensor_tensor(out=part, in0=part, in1=whole_turns[:], op=ALU.subtract)
-
-
-def sines_and_cosines(nc, setup, keep, angle):
-    table = keep.tile([P, TILES, 2, FREQS], F32, name="table")
-    for start in range(0, TILES, TABLE_STEP):
-        part = angle[:, start : start + TABLE_STEP, :]
-        nc.scalar.activation(
-            out=table[:, start : start + TABLE_STEP, 1, :], in_=part, func=ACT.Sin,
-            scale=2.0 * math.pi,
-        )
-        half_sine = setup.tile([P, TABLE_STEP, FREQS], F32, tag="half_sine", bufs=2)
-        nc.scalar.activation(out=half_sine[:], in_=part, func=ACT.Sin, scale=math.pi)
-        nc.vector.tensor_tensor(out=half_sine[:], in0=half_sine[:], in1=half_sine[:], op=ALU.mult)
-        nc.gpsimd.tensor_scalar(
-            out=table[:, start : start + TABLE_STEP, 0, :], in0=half_sine[:],
-            scalar1=-2.0, scalar2=1.0, op0=ALU.mult, op1=ALU.add,
-        )
-    return table
 
 
 def tile_transformerlayershard_pa_t_kernel(
@@ -207,216 +57,390 @@ def tile_transformerlayershard_pa_t_kernel(
     with ExitStack() as ctx:
         keep = ctx.enter_context(tc.tile_pool(name="keep", bufs=1))
         setup = ctx.enter_context(tc.tile_pool(name="setup", bufs=1))
-        loads = ctx.enter_context(tc.tile_pool(name="loads", bufs=LOADS_AHEAD))
-        stats = ctx.enter_context(tc.tile_pool(name="stats", bufs=4))
-        work = ctx.enter_context(tc.tile_pool(name="work", bufs=2))
-        banks = ctx.enter_context(tc.psum_pool(name="banks", bufs=PSUM_BANKS - GROUP - 1))
-        qk_banks = ctx.enter_context(tc.psum_pool(name="qk_banks", bufs=GROUP))
+        loads = ctx.enter_context(tc.tile_pool(name="loads", bufs=X_BUFS))
+        stats = ctx.enter_context(tc.tile_pool(name="stats", bufs=8))
+        work = ctx.enter_context(tc.tile_pool(name="work", bufs=3))
+        turned_banks = ctx.enter_context(tc.psum_pool(name="turned_banks", bufs=5))
+        qk_banks = ctx.enter_context(tc.psum_pool(name="qk_banks", bufs=2))
         v_banks = ctx.enter_context(tc.psum_pool(name="v_banks", bufs=1))
         ctx.enter_context(tc.manual_schedule())
 
-        x_of, neg_mean_of, spread_of, y_of, planes_of = {}, {}, {}, {}, {}
-        codes_of, scales_of, qk_acc_of, v_acc_of, products_of = {}, {}, {}, {}, {}
-        shared = {}
+        x_of, sums_of, neg_mean_of, squares_of, y_of = {}, {}, {}, {}, {}
+        turned_of, grouped_of, codes_of, scales_of = {}, {}, {}, {}
+        qk_acc_of, v_acc_of, products_of, parts_of = {}, {}, {}, {}
 
-        def load(n):
-            x_g = loads.tile([P, GROUP, D], BF16, tag="x_g")
-            nc.sync.dma_start(out=x_g[:], in_=x_rows[:, n * GROUP : (n + 1) * GROUP, :])
-            x_of[n] = x_g
 
-        def row_sums(n):
-            sums = stats.tile([P, GROUP], F32, tag="sums")
-            for t in range(GROUP):
-                unread_v = work.tile([P, D], BF16, tag="unread_v")
+        def load(u):
+            x_u = loads.tile([P, UNIT, D], BF16, tag="x_u", name="x_u")
+            if u == 0:
+                for t in range(UNIT):
+                    nc.sync.dma_start(out=x_u[:, t, :], in_=x_rows[:, t, :])
+            else:
+                nc.sync.dma_start(out=x_u[:], in_=x_rows[:, u * UNIT : (u + 1) * UNIT, :])
+            for t in range(UNIT):
+                x_of[u * UNIT + t] = x_u[:, t, :]
+
+        def row_sum(n):
+            sums_of[n] = stats.tile([P, 1], F32, tag="sums", name="sums")
+            if n < HEAD_TILES or n % VECTOR_SUM_EVERY == 1:
+                unread_v = work.tile([P, D], BF16, tag="unread_v", name="unread_v")
                 nc.vector.tensor_scalar(
-                    out=unread_v[:], in0=x_of[n][:, t, :], scalar1=1.0, scalar2=None,
-                    op0=ALU.mult, op1=ALU.add, accum_out=sums[:, t : t + 1],
+                    out=unread_v[:], in0=x_of[n], scalar1=1.0, scalar2=None,
+                    op0=ALU.mult, op1=ALU.add, accum_out=sums_of[n][:],
                 )
-            neg_mean = stats.tile([P, GROUP], F32, tag="neg_mean")
-            nc.vector.tensor_scalar(
-                out=neg_mean[:], in0=sums[:], scalar1=-1.0 / D, scalar2=None, op0=ALU.mult
-            )
+            else:
+                unread_s = work.tile([P, D], BF16, tag="unread_s", name="unread_s")
+                nc.scalar.activation(
+                    out=unread_s[:], in_=x_of[n], func=ACT.Copy, scale=1.0, accum_out=sums_of[n][:]
+                )
+
+        def negate_mean(n):
+            neg_mean = stats.tile([P, 1], F32, tag="neg_mean", name="neg_mean")
+            nc.scalar.activation(out=neg_mean[:], in_=sums_of[n][:], func=ACT.Copy, scale=-1.0 / D)
             neg_mean_of[n] = neg_mean
 
-        def row_spread(n):
-            squares = stats.tile([P, GROUP], F32, tag="squares")
-            for t in range(GROUP):
-                unread_s = work.tile([P, D], BF16, tag="unread_s")
-                nc.scalar.activation(
-                    out=unread_s[:], in_=x_of[n][:, t, :], func=ACT.Square,
-                    bias=neg_mean_of[n][:, t : t + 1], scale=1.0,
-                    accum_out=squares[:, t : t + 1],
-                )
-            spread = stats.tile([P, GROUP], F32, tag="spread")
+        def row_squares(n):
+            squares_of[n] = stats.tile([P, 1], F32, tag="squares", name="squares")
+            unread_s = work.tile([P, D], BF16, tag="unread_s", name="unread_s")
             nc.scalar.activation(
-                out=spread[:], in_=squares[:], func=ACT.Sqrt, scale=1.0 / D,
-                bias=shared["eps"][:, 0:1],
+                out=unread_s[:], in_=x_of[n], func=ACT.Square, bias=neg_mean_of[n][:, 0:1], scale=1.0,
+                accum_out=squares_of[n][:],
             )
-            spread_of[n] = spread
 
         def normalise(n):
-            rstd = stats.tile([P, GROUP], F32, tag="rstd")
-            nc.vector.reciprocal(out=rstd[:], in_=spread_of[n][:])
-            y_g = work.tile([P, GROUP, D], F32, tag="y_g")
-            for t in range(GROUP):
-                nc.gpsimd.tensor_scalar(
-                    out=y_g[:, t, :].rearrange("r (h j p) -> r h j p", h=PASSES, j=PACK),
-                    in0=x_of[n][:, t, :].rearrange("r (h p j) -> r h j p", p=P, j=PACK),
-                    scalar1=neg_mean_of[n][:, t : t + 1], scalar2=rstd[:, t : t + 1],
-                    op0=ALU.add, op1=ALU.mult,
-                )
-            y_of[n] = y_g
+            variance = stats.tile([P, 1], F32, tag="variance", name="variance")
+            nc.gpsimd.tensor_scalar(
+                out=variance[:], in0=squares_of[n][:], scalar1=1.0 / D, scalar2=EPS,
+                op0=ALU.mult, op1=ALU.add,
+            )
+            rstd = stats.tile([P, 1], F32, tag="rstd", name="rstd")
+            nc.gpsimd.tensor_tensor(
+                out=rstd[:], in0=variance[:], in1=minus_half[:], op=ALU.pow
+            )
+            y_n = work.tile([P, PASSES, PACK, P], F32, tag="y_n", name="y_n")
+            engine = nc.vector if n < 2 else nc.gpsimd
+            engine.tensor_scalar(
+                out=y_n[:], in0=x_of[n].rearrange("r (h p j) -> r h j p", p=P, j=PACK),
+                scalar1=neg_mean_of[n][:, 0:1], scalar2=rstd[:, 0:1], op0=ALU.add, op1=ALU.mult,
+            )
+            y_of[n] = y_n
 
         def turn(n):
-            gain_bias = shared["gain_bias"]
-            planes = work.tile([P, CHUNKS, ROWS], BF16, tag="planes")
-            for c in range(CHUNKS):
-                turned = banks.tile([P, ROWS], F32, tag="turned")
-                for t in range(GROUP):
-                    nc.tensor.transpose(
-                        turned[:, t * P : (t + 1) * P], y_of[n][:, t, c * P : (c + 1) * P],
-                        shared["ident"][:],
+            for h in range(PASSES):
+                turned = turned_banks.tile([P, PACK, P], F32, tag="turned", name="turned")
+                for j in range(PACK):
+                    nc.tensor.matmul(
+                        turned[:, j, :], lhsT=y_of[n][:, h, j, :], rhs=ident[:],
+                        is_transpose=True, start=True, stop=False,
                     )
-                nc.scalar.activation(
-                    out=planes[:, c, :], in_=turned[:], func=ACT.Identity,
-                    scale=gain_bias[:, c : c + 1], bias=gain_bias[:, CHUNKS + c : CHUNKS + c + 1],
-                )
-            planes_of[n] = planes
+                    nc.tensor.matmul(
+                        turned[:, j, :], lhsT=offset_rows[:, h, j, :], rhs=ident[:],
+                        is_transpose=True, start=False, stop=True,
+                    )
+                turned_of[(n, h)] = turned
 
-        def pack(n):
-            grouped = work.tile([P, PASSES, ROWS, PACK], BF16, tag="grouped", bufs=1, align_bytes=64)
-            codes = work.tile([P, PASSES, ROWS], U32, tag="codes", align_bytes=64)
-            scales = work.tile([P, PASSES, ROWS], U8, tag="scales", align_bytes=64)
-            for h in range(PASSES):
-                nc.vector.tensor_copy(
-                    out=grouped[:, h, :, :].rearrange("p (w i) j -> p w j i", i=4),
-                    in_=planes_of[n][:, h * PACK : (h + 1) * PACK, :].rearrange(
-                        "p j (w i) -> p w j i", i=4
-                    ),
-                )
-            for h in range(PASSES):
-                nc.vector.quantize_mx(
-                    out=codes[:, h, :].bitcast(FP8X4),
-                    scales=scales[:, h, :],
-                    in_=grouped[:, h, :, :].rearrange("p w j -> p (w j)"),
-                )
-            codes_of[n] = codes
-            scales_of[n] = scales
-
-        def project_tile(n, t):
-            qk_codes, qk_scales, v_codes, v_scales = shared["weights"]
-            codes, scales = codes_of[n], scales_of[n]
-            rows = slice(t * P, (t + 1) * P)
+        def gain(n):
+            u, t = n // UNIT, n % UNIT
             if t == 0:
-                v_acc_of[n] = v_banks.tile([P, GROUP * DH], F32, tag="v_acc", name="v_acc")
-            qk_acc = qk_banks.tile([P, BANK], F32, tag="qk_acc")
-            for h in range(PASSES):
-                nc.tensor.matmul_mx(
-                    out=qk_acc[:],
-                    lhsT=codes[:, h, rows].bitcast(FP8X4),
-                    lhsT_scale=scales[:, h, rows],
-                    rhs=qk_codes[:, h, :].bitcast(FP8X4),
-                    rhs_scale=qk_scales[:, h, :],
-                    start=(h == 0),
-                    stop=(h == PASSES - 1),
+                grouped_of[u] = work.tile(
+                    [P, UNIT, PASSES, P, PACK], BF16, tag="grouped", name="grouped",
+                    align_bytes=64,
                 )
             for h in range(PASSES):
-                nc.tensor.matmul_mx(
-                    out=v_acc_of[n][:, rows],
-                    lhsT=codes[:, h, rows].bitcast(FP8X4),
-                    lhsT_scale=scales[:, h, rows],
-                    rhs=v_codes[:, h, :].bitcast(FP8X4),
-                    rhs_scale=v_scales[:, h, :],
-                    start=(h == 0),
-                    stop=(h == PASSES - 1),
+                nc.vector.tensor_tensor(
+                    out=grouped_of[u][:, t, h, :, :],
+                    in0=turned_of[(n, h)][:].rearrange("p j r -> p r j"),
+                    in1=gains[:, h, :].unsqueeze(1).to_broadcast([P, P, PACK]),
+                    op=ALU.mult,
                 )
-            qk_acc_of[(n, t)] = qk_acc
 
-        def rotate_tile(n, t):
-            if t == 0:
-                products_of[n] = work.tile(
-                    [P, GROUP, 4, DH], F32, tag="products", name="products", bufs=1
-                )
+
+        def quantise(u):
+            codes = work.tile([P, UNIT, PASSES, P], U32, tag="codes", name="codes", align_bytes=64)
+            scales = work.tile([P, UNIT, PASSES, P], U8, tag="scales", name="scales", align_bytes=64)
+            nc.vector.quantize_mx(
+                out=codes[:].rearrange("p t h r -> p (t h r)").bitcast(FP8X4),
+                scales=scales[:].rearrange("p t h r -> p (t h r)"),
+                in_=grouped_of[u][:].rearrange("p t h r j -> p (t h r j)"),
+            )
+            codes_of[u] = codes
+            scales_of[u] = scales
+
+        def project(u):
+            codes, scales = codes_of[u], scales_of[u]
+            qk_acc = qk_banks.tile([P, UNIT, 2 * DH], F32, tag="qk_acc", name="qk_acc")
+            v_acc = v_banks.tile([P, UNIT, DH], F32, tag="v_acc", name="v_acc")
+            for acc, w_codes, w_scales in ((qk_acc, qk_codes, qk_scales), (v_acc, v_codes, v_scales)):
+                for t in range(UNIT):
+                    for h in range(PASSES):
+                        nc.tensor.matmul_mx(
+                            out=acc[:, t, :],
+                            lhsT=codes[:, t, h, :].bitcast(FP8X4),
+                            lhsT_scale=scales[:, t, h, :],
+                            rhs=w_codes[:, h, :].bitcast(FP8X4),
+                            rhs_scale=w_scales[:, h, :],
+                            start=(h == 0),
+                            stop=(h == PASSES - 1),
+                        )
+            qk_acc_of[u] = qk_acc
+            v_acc_of[u] = v_acc
+
+        def rotate(u):
+            tiles = slice(u * UNIT, (u + 1) * UNIT)
+            shape = [P, UNIT, 2, 4, FREQS]
+            products = work.tile([P, UNIT, 2, 2 * DH], F32, tag="products", name="products")
             nc.vector.tensor_tensor(
-                out=products_of[n][:, t, :, :],
-                in0=qk_acc_of[(n, t)][:].rearrange("p (a w) -> p a w", a=4),
-                in1=shared["table"][:, n * GROUP + t, :, :]
-                .rearrange("p s c -> p (s c)")
-                .unsqueeze(1)
-                .to_broadcast([P, 4, DH]),
+                out=products[:].rearrange("p t s (g c) -> p t s g c", c=FREQS),
+                in0=qk_acc_of[u][:].rearrange("p t (g c) -> p t g c", c=FREQS)
+                .unsqueeze(2).to_broadcast(shape),
+                in1=table[:, tiles, :, :].unsqueeze(3).to_broadcast(shape),
                 op=ALU.mult,
             )
+            products_of[u] = products
 
-        def store_qk(n):
-            tiles = slice(n * GROUP, (n + 1) * GROUP)
-            products = products_of[n]
-            qk_out = work.tile([P, GROUP, 2, DH], F32, tag="qk_out")
+        def store_qk(u):
+            tiles, products = slice(u * UNIT, (u + 1) * UNIT), products_of[u]
+            qk_out = work.tile([P, 2, UNIT, DH], F32, tag="qk_out", name="qk_out")
             nc.vector.tensor_tensor(
-                out=qk_out[:].rearrange("p t g (r c) -> p (t g r) c", r=2),
-                in0=products[:, :, :, 0:FREQS].rearrange("p t a c -> p (t a) c"),
-                in1=products[:, :, :, FREQS:DH].rearrange("p t a c -> p (t a) c"),
+                out=qk_out[:].rearrange("p g t (i e) -> p t g i e", e=2),
+                in0=products[:, :, 0, :].rearrange("p t (g i e) -> p t g i e", g=2, e=2),
+                in1=products[:, :, 1, :].rearrange("p t (g i e) -> p t g i e", g=2, e=2)[
+                    :, :, :, :, ::-1
+                ],
                 op=ALU.add,
             )
-            nc.sync.dma_start(out=q_rows[:, tiles, :], in_=qk_out[:, :, 0, :])
-            nc.sync.dma_start(out=k_rows[:, tiles, :], in_=qk_out[:, :, 1, :])
+            nc.sync.dma_start(out=q_rows[:, tiles, :], in_=qk_out[:, 0, :, :])
+            nc.sync.dma_start(out=k_rows[:, tiles, :], in_=qk_out[:, 1, :, :])
 
-        def store_v(n):
-            tiles = slice(n * GROUP, (n + 1) * GROUP)
-            v_out = work.tile([P, GROUP, DH], F32, tag="v_out")
-            nc.vector.tensor_copy(out=v_out[:].rearrange("p t j -> p (t j)"), in_=v_acc_of[n][:])
-            nc.sync.dma_start(out=v_rows[:, tiles, :], in_=v_out[:])
+        def store_v(u):
+            v_out = work.tile([P, UNIT, DH], F32, tag="v_out", name="v_out")
+            nc.scalar.copy(out=v_out[:], in_=v_acc_of[u][:])
+            nc.sync.dma_start(out=v_rows[:, u * UNIT : (u + 1) * UNIT, :], in_=v_out[:])
 
-        def live(n):
-            return 0 <= n < GROUPS
+        def table_angles(g):
+            shape = [P, STEP, FREQS]
+            angle = work.tile(shape, F32, tag="angle", name="angle")
+            nc.vector.scalar_tensor_tensor(
+                out=angle[:], in0=turns[:].unsqueeze(1).to_broadcast(shape),
+                scalar=float(STEP * g), in1=first_angles[:], op0=ALU.mult, op1=ALU.add,
+            )
+            whole = work.tile(shape, F32, tag="whole", name="whole")
+            nc.vector.tensor_scalar(
+                out=whole[:], in0=angle[:], scalar1=ROUND_MAGIC, scalar2=ROUND_MAGIC,
+                op0=ALU.add, op1=ALU.subtract,
+            )
+            part = work.tile(shape, F32, tag="part", name="part")
+            nc.vector.tensor_tensor(out=part[:], in0=angle[:], in1=whole[:], op=ALU.subtract)
+            parts_of[g] = part
 
-        def one_round(i):
-            if live(i + 5) and i + 5 >= LOADS_AHEAD:
-                load(i + 5)
-            if live(i + 1):
-                turn(i + 1)
-            if live(i):
-                pack(i)
-            if live(i - 2):
-                store_qk(i - 2)
-            if live(i + 2):
-                normalise(i + 2)
-            if live(i - 1):
-                store_v(i - 1)
-            for t in range(GROUP):
-                if live(i - 1):
-                    rotate_tile(i - 1, t)
-                if live(i):
-                    project_tile(i, t)
-            if live(i + 3):
-                row_spread(i + 3)
-            if live(i + 4):
-                row_sums(i + 4)
+        def table_values(g):
+            tiles, part = slice(g * STEP, (g + 1) * STEP), parts_of[g]
+            nc.scalar.activation(
+                out=table[:, tiles, 1, :].rearrange("p t (i e) -> p t i e", e=2),
+                in_=part[:].rearrange("p t (i e) -> p t i e", e=2)[:, :, :, ::-1],
+                func=ACT.Sin, scale=2.0 * math.pi,
+            )
+            size = work.tile([P, STEP, FREQS], F32, tag="size", name="size")
+            nc.scalar.activation(out=size[:], in_=part[:], func=ACT.Abs)
+            nc.scalar.activation(
+                out=table[:, tiles, 0, :], in_=size[:], func=ACT.Sin, scale=-2.0 * math.pi,
+                bias=quarter[:, 0:1],
+            )
 
-        for n in range(LOADS_AHEAD):
-            load(n)
+
+        scale_cols = setup.tile([P, PASSES, PACK], BF16, name="scale_cols")
+        nc.sync.dma_start(
+            out=scale_cols[:], in_=ln_scale.rearrange("(h p j) -> p h j", p=P, j=PACK)
+        )
+        offset_cols = setup.tile([P, PASSES, PACK], BF16, name="offset_cols")
+        nc.sync.dma_start(
+            out=offset_cols[:], in_=ln_offset.rearrange("(h p j) -> p h j", p=P, j=PACK)
+        )
+        load(0)
+        load(1)
+        raws = []
+        for name, w in (("w_raw_q", Wq), ("w_raw_k", Wk), ("w_raw_v", Wv)):
+            raw = setup.tile([P, PASSES, PACK, DH], BF16, name=name)
+            nc.sync.dma_start(
+                out=raw[:], in_=w.rearrange("(h p j) n -> p h j n", p=P, j=PACK)
+            )
+            raws.append(raw)
+        for u in range(2, 5):
+            load(u)
+
         ident = keep.tile([P, P], F32, name="ident")
         make_identity(nc, ident[:])
-        shared["ident"] = ident
         first_i = setup.tile([P, 1], I32, name="first_i")
         nc.gpsimd.iota(first_i[:], pattern=[[0, 1]], base=0, channel_multiplier=TILES)
         one = setup.tile([P, 1], F32, name="one")
         nc.vector.memset(one[:], 1.0)
-        eps = keep.tile([P, 1], F32, name="eps")
-        nc.vector.tensor_scalar(out=eps[:], in0=one[:], scalar1=EPS, scalar2=None, op0=ALU.mult)
-        shared["eps"] = eps
-        turns_lo = fine_frequencies(nc, setup, one)
-        one_round(-4)
-        one_round(-3)
-        shared["gain_bias"] = load_layer_norm_columns(
-            nc, setup, keep, banks, ident, ln_scale, ln_offset
+        minus_half = keep.tile([P, 1], F32, name="minus_half")
+        nc.vector.memset(minus_half[:], -0.5)
+        quarter = keep.tile([P, 1], F32, name="quarter")
+        nc.vector.tensor_scalar(
+            out=quarter[:], in0=one[:], scalar1=math.pi / 2.0, scalar2=None, op0=ALU.mult
         )
-        one_round(-2)
-        turns_hi = coarse_frequencies(nc, setup)
-        angle = first_angles(nc, setup, first_i, turns_hi, turns_lo)
-        one_round(-1)
-        all_angles(nc, setup, angle, turns_hi, turns_lo)
-        shared["weights"] = quantise_weights(nc, setup, keep, Wq, Wk, Wv)
-        one_round(0)
-        shared["table"] = sines_and_cosines(nc, setup, keep, angle)
-        for i in range(1, GROUPS + 2):
-            one_round(i)
+        turns_hi = setup.tile([P, DECADE], F32, name="turns_hi")
+        turns_lo = setup.tile([P, DECADE], F32, name="turns_lo")
+        for c in range(DECADE):
+            hi, lo = turns_per_position(c)
+            nc.gpsimd.memset(turns_hi[:, c : c + 1], hi)
+            nc.vector.tensor_scalar(
+                out=turns_lo[:, c : c + 1], in0=one[:], scalar1=lo, scalar2=None, op0=ALU.mult
+            )
+        turns = keep.tile([P, FREQS], F32, name="turns")
+        nc.gpsimd.tensor_tensor(
+            out=turns[:, 0:DECADE], in0=turns_hi[:], in1=turns_lo[:], op=ALU.add
+        )
+        for d in range(1, FREQS // DECADE):
+            nc.gpsimd.tensor_scalar(
+                out=turns[:, d * DECADE : (d + 1) * DECADE], in0=turns[:, 0:DECADE],
+                scalar1=10.0 ** -d, scalar2=0.0, op0=ALU.mult, op1=ALU.add,
+            )
+
+        gains = keep.tile([P, PASSES, PACK], F32, name="gains")
+        small = setup.tile([P, PASSES, PACK], F32, name="small")
+        nc.vector.tensor_tensor(
+            out=small[:], in0=scale_cols[:], in1=scale_cols[:], op=ALU.mult
+        )
+        row_sum(0)
+        negate_mean(0)
+        nc.vector.tensor_scalar(
+            out=small[:], in0=small[:], scalar1=TINY * TINY, scalar2=TINY,
+            op0=ALU.is_lt, op1=ALU.mult,
+        )
+        row_squares(0)
+        nc.vector.tensor_tensor(
+            out=gains[:], in0=scale_cols[:], in1=small[:], op=ALU.add
+        )
+        row_sum(1)
+        negate_mean(1)
+        ratio = setup.tile([P, PASSES, PACK], F32, name="ratio")
+        nc.vector.reciprocal(out=ratio[:], in_=gains[:])
+        nc.vector.tensor_tensor(
+            out=ratio[:], in0=ratio[:], in1=offset_cols[:], op=ALU.mult
+        )
+        ratio_cols = setup.tile([P, SLOTS, P], F32, name="ratio_cols")
+        nc.vector.tensor_copy(
+            out=ratio_cols[:],
+            in_=ratio[:].rearrange("p h j -> p (h j)").unsqueeze(2).to_broadcast([P, SLOTS, P]),
+        )
+        offset_rows = keep.tile([P, PASSES, PACK, P], F32, name="offset_rows")
+        for h in range(PASSES):
+            turned_ratio = turned_banks.tile([P, PACK, P], F32, tag="turned", name="turned_ratio")
+            for j in range(PACK):
+                nc.tensor.transpose(
+                    turned_ratio[:, j, :], ratio_cols[:, h * PACK + j, :], ident[:]
+                )
+            nc.scalar.copy(out=offset_rows[:, h, :, :], in_=turned_ratio[:])
+        row_squares(1)
+
+        qk_grouped = setup.tile([P, PASSES, 2 * DH, PACK], BF16, name="qk_grouped", align_bytes=64)
+        v_grouped = setup.tile([P, PASSES, DH, PACK], BF16, name="v_grouped", align_bytes=64)
+        for h in range(PASSES):
+            for g in range(2):
+                nc.vector.tensor_copy(
+                    out=qk_grouped[:, h, g * DH : (g + 1) * DH, :],
+                    in_=raws[g][:, h, :, :].rearrange("p j n -> p n j"),
+                )
+        normalise(0)
+        turn(0)
+        row_sum(2)
+        negate_mean(2)
+        row_squares(2)
+        for h in range(PASSES):
+            nc.vector.tensor_copy(
+                out=v_grouped[:, h, :, :], in_=raws[2][:, h, :, :].rearrange("p j n -> p n j")
+            )
+        normalise(1)
+        row_sum(3)
+        negate_mean(3)
+        qk_codes = keep.tile([P, PASSES, 2 * DH], U32, name="qk_codes", align_bytes=64)
+        qk_scales = keep.tile([P, PASSES, 2 * DH], U8, name="qk_scales", align_bytes=64)
+        v_codes = keep.tile([P, PASSES, DH], U32, name="v_codes", align_bytes=64)
+        v_scales = keep.tile([P, PASSES, DH], U8, name="v_scales", align_bytes=64)
+
+        def quantise_weights():
+            nc.vector.quantize_mx(
+                out=qk_codes[:].rearrange("p h n -> p (h n)").bitcast(FP8X4),
+                scales=qk_scales[:].rearrange("p h n -> p (h n)"),
+                in_=qk_grouped[:].rearrange("p h n j -> p (h n j)"),
+            )
+            nc.vector.quantize_mx(
+                out=v_codes[:].rearrange("p h n -> p (h n)").bitcast(FP8X4),
+                scales=v_scales[:].rearrange("p h n -> p (h n)"),
+                in_=v_grouped[:].rearrange("p h n j -> p (h n j)"),
+            )
+
+        table = keep.tile([P, TILES, 2, FREQS], F32, name="table")
+        first_angles = keep.tile([P, STEP, FREQS], F32, name="first_angles")
+
+        def start_angles():
+            first = setup.tile([P, 1], F32, name="first")
+            nc.vector.tensor_copy(out=first[:], in_=first_i[:])
+            start = setup.tile([P, FREQS], F32, name="start")
+            nc.vector.tensor_scalar(
+                out=start[:, 0:DECADE], in0=turns_hi[:], scalar1=first[:, 0:1], scalar2=None,
+                op0=ALU.mult,
+            )
+            nc.vector.tensor_scalar(
+                out=start[:, DECADE:FREQS], in0=turns[:, DECADE:FREQS], scalar1=first[:, 0:1],
+                scalar2=None, op0=ALU.mult,
+            )
+            start_whole = setup.tile([P, FREQS], F32, name="start_whole")
+            nc.vector.tensor_scalar(
+                out=start_whole[:], in0=start[:], scalar1=ROUND_MAGIC, scalar2=ROUND_MAGIC,
+                op0=ALU.add, op1=ALU.subtract,
+            )
+            nc.vector.tensor_tensor(
+                out=first_angles[:, 0, :], in0=start[:], in1=start_whole[:], op=ALU.subtract
+            )
+            nc.vector.scalar_tensor_tensor(
+                out=first_angles[:, 0, 0:DECADE], in0=turns_lo[:], scalar=first[:, 0:1],
+                in1=first_angles[:, 0, 0:DECADE], op0=ALU.mult, op1=ALU.add,
+            )
+            for i in range(1, STEP):
+                nc.vector.scalar_tensor_tensor(
+                    out=first_angles[:, i, :], in0=turns[:], scalar=float(i),
+                    in1=first_angles[:, 0, :], op0=ALU.mult, op1=ALU.add,
+                )
+
+
+        def live(n):
+            return 0 <= n < TILES
+
+        for k in range(TILES + 2):
+            u = k // UNIT
+            if k % UNIT == 0 and u + 4 < UNITS and u > 0:
+                load(u + 4)
+            if k % UNIT == 0 and u > 0:
+                project(u - 1)
+            if live(k):
+                gain(k)
+            if k == 0:
+                quantise_weights()
+                start_angles()
+                table_angles(0)
+                table_values(0)
+            if live(k + 4):
+                row_sum(k + 4)
+            if k % UNIT == 0 and u > 0:
+                rotate(u - 1)
+            if k % UNIT == 1 and u > 0:
+                store_qk(u - 1)
+            if k % UNIT == 1 and live(k):
+                quantise(u)
+            if live(k + 1):
+                turn(k + 1)
+            if live(k + 2):
+                normalise(k + 2)
+            if live(k + 3):
+                row_squares(k + 3)
+            if live(k + 4):
+                negate_mean(k + 4)
+            if k % UNIT == 0 and u > 0:
+                store_v(u - 1)
+            if k % STEP == 1 and live(k + 3):
+                table_angles((k + 3) // STEP)
+            if k % STEP == 2 and live(k + 2):
+                table_values((k + 2) // STEP)

@@ -33,6 +33,7 @@ STEP = 4
 TINY = 2.0 ** -60
 HEAD_TILES = 4
 VECTOR_SUM_EVERY = 6
+WARM_COLS = 32
 X_BUFS = 8
 
 FLOPS = 2 * S * D * 3 * DH
@@ -128,6 +129,10 @@ def tile_transformerlayershard_pa_t_kernel(
         def turn(n):
             for h in range(PASSES):
                 turned = turned_banks.tile([P, PACK, P], F32, tag="turned", name="turned")
+                nc.tensor.matmul(
+                    turned[:, 0, 0:WARM_COLS], lhsT=ident[:], rhs=ident[:, 0:WARM_COLS],
+                    start=True, stop=True,
+                )
                 for j in range(PACK):
                     nc.tensor.matmul(
                         turned[:, j, :], lhsT=y_of[n][:, h, j, :], rhs=ident[:],
@@ -166,51 +171,50 @@ def tile_transformerlayershard_pa_t_kernel(
             codes_of[u] = codes
             scales_of[u] = scales
 
-        def project(u):
+        def project(n):
+            u, t = n // UNIT, n % UNIT
             codes, scales = codes_of[u], scales_of[u]
-            qk_acc = qk_banks.tile([P, UNIT, 2 * DH], F32, tag="qk_acc", name="qk_acc")
-            v_acc = v_banks.tile([P, UNIT, DH], F32, tag="v_acc", name="v_acc")
-            for acc, w_codes, w_scales in ((qk_acc, qk_codes, qk_scales), (v_acc, v_codes, v_scales)):
-                for t in range(UNIT):
-                    for h in range(PASSES):
-                        nc.tensor.matmul_mx(
-                            out=acc[:, t, :],
-                            lhsT=codes[:, t, h, :].bitcast(FP8X4),
-                            lhsT_scale=scales[:, t, h, :],
-                            rhs=w_codes[:, h, :].bitcast(FP8X4),
-                            rhs_scale=w_scales[:, h, :],
-                            start=(h == 0),
-                            stop=(h == PASSES - 1),
-                        )
-            qk_acc_of[u] = qk_acc
-            v_acc_of[u] = v_acc
+            qk_acc = qk_banks.tile([P, BANK], F32, tag="qk_acc", name="qk_acc")
+            if t == 0:
+                v_acc_of[u] = v_banks.tile([P, UNIT, DH], F32, tag="v_acc", name="v_acc")
+            for acc, w_codes, w_scales in (
+                (qk_acc[:], qk_codes, qk_scales), (v_acc_of[u][:, t, :], v_codes, v_scales)
+            ):
+                for h in range(PASSES):
+                    nc.tensor.matmul_mx(
+                        out=acc,
+                        lhsT=codes[:, t, h, :].bitcast(FP8X4),
+                        lhsT_scale=scales[:, t, h, :],
+                        rhs=w_codes[:, h, :].bitcast(FP8X4),
+                        rhs_scale=w_scales[:, h, :],
+                        start=(h == 0),
+                        stop=(h == PASSES - 1),
+                    )
+            qk_acc_of[n] = qk_acc
 
-        def rotate(u):
-            tiles = slice(u * UNIT, (u + 1) * UNIT)
-            shape = [P, UNIT, 2, 4, FREQS]
-            products = work.tile([P, UNIT, 2, 2 * DH], F32, tag="products", name="products")
+        def rotate(n):
+            u, t = n // UNIT, n % UNIT
+            if t == 0:
+                products_of[u] = work.tile([P, UNIT, 4, DH], F32, tag="products", name="products")
             nc.vector.tensor_tensor(
-                out=products[:].rearrange("p t s (g c) -> p t s g c", c=FREQS),
-                in0=qk_acc_of[u][:].rearrange("p t (g c) -> p t g c", c=FREQS)
-                .unsqueeze(2).to_broadcast(shape),
-                in1=table[:, tiles, :, :].unsqueeze(3).to_broadcast(shape),
+                out=products_of[u][:, t, :, :],
+                in0=qk_acc_of[n][:].rearrange("p (a w) -> p a w", a=4),
+                in1=table[:, n, :, :].rearrange("p s c -> p (s c)").unsqueeze(1)
+                .to_broadcast([P, 4, DH]),
                 op=ALU.mult,
             )
-            products_of[u] = products
 
         def store_qk(u):
             tiles, products = slice(u * UNIT, (u + 1) * UNIT), products_of[u]
-            qk_out = work.tile([P, 2, UNIT, DH], F32, tag="qk_out", name="qk_out")
+            qk_out = work.tile([P, UNIT, 2, DH], F32, tag="qk_out", name="qk_out")
             nc.vector.tensor_tensor(
-                out=qk_out[:].rearrange("p g t (i e) -> p t g i e", e=2),
-                in0=products[:, :, 0, :].rearrange("p t (g i e) -> p t g i e", g=2, e=2),
-                in1=products[:, :, 1, :].rearrange("p t (g i e) -> p t g i e", g=2, e=2)[
-                    :, :, :, :, ::-1
-                ],
+                out=qk_out[:].rearrange("p t g (r c) -> p (t g r) c", r=2),
+                in0=products[:, :, :, 0:FREQS].rearrange("p t a c -> p (t a) c"),
+                in1=products[:, :, :, FREQS:DH].rearrange("p t a c -> p (t a) c"),
                 op=ALU.add,
             )
-            nc.sync.dma_start(out=q_rows[:, tiles, :], in_=qk_out[:, 0, :, :])
-            nc.sync.dma_start(out=k_rows[:, tiles, :], in_=qk_out[:, 1, :, :])
+            nc.sync.dma_start(out=q_rows[:, tiles, :], in_=qk_out[:, :, 0, :])
+            nc.sync.dma_start(out=k_rows[:, tiles, :], in_=qk_out[:, :, 1, :])
 
         def store_v(u):
             v_out = work.tile([P, UNIT, DH], F32, tag="v_out", name="v_out")
@@ -236,8 +240,7 @@ def tile_transformerlayershard_pa_t_kernel(
         def table_values(g):
             tiles, part = slice(g * STEP, (g + 1) * STEP), parts_of[g]
             nc.scalar.activation(
-                out=table[:, tiles, 1, :].rearrange("p t (i e) -> p t i e", e=2),
-                in_=part[:].rearrange("p t (i e) -> p t i e", e=2)[:, :, :, ::-1],
+                out=table[:, tiles, 1, :], in_=part[:],
                 func=ACT.Sin, scale=2.0 * math.pi,
             )
             size = work.tile([P, STEP, FREQS], F32, tag="size", name="size")
@@ -335,14 +338,24 @@ def tile_transformerlayershard_pa_t_kernel(
             nc.scalar.copy(out=offset_rows[:, h, :, :], in_=turned_ratio[:])
         row_squares(1)
 
-        qk_grouped = setup.tile([P, PASSES, 2 * DH, PACK], BF16, name="qk_grouped", align_bytes=64)
+        qk_grouped = setup.tile([P, PASSES, BANK, PACK], BF16, name="qk_grouped", align_bytes=64)
         v_grouped = setup.tile([P, PASSES, DH, PACK], BF16, name="v_grouped", align_bytes=64)
         for h in range(PASSES):
             for g in range(2):
+                cols = qk_grouped[:, h, g * 2 * DH : (g + 1) * 2 * DH, :]
                 nc.vector.tensor_copy(
-                    out=qk_grouped[:, h, g * DH : (g + 1) * DH, :],
-                    in_=raws[g][:, h, :, :].rearrange("p j n -> p n j"),
+                    out=cols.rearrange("p (r s c) j -> p r s c j", r=2, s=2)[:, :, 0, :, :],
+                    in_=raws[g][:, h, :, :].rearrange("p j (r c) -> p r c j", r=2),
                 )
+                for a in range(2):
+                    nc.vector.tensor_copy(
+                        out=cols.rearrange("p (r s i e) j -> p r s i e j", r=2, s=2, e=2)[
+                            :, :, 1, :, a, :
+                        ],
+                        in_=raws[g][:, h, :, :].rearrange("p j (r i e) -> p r i e j", r=2, e=2)[
+                            :, :, :, 1 - a, :
+                        ],
+                    )
         normalise(0)
         turn(0)
         row_sum(2)
@@ -355,8 +368,8 @@ def tile_transformerlayershard_pa_t_kernel(
         normalise(1)
         row_sum(3)
         negate_mean(3)
-        qk_codes = keep.tile([P, PASSES, 2 * DH], U32, name="qk_codes", align_bytes=64)
-        qk_scales = keep.tile([P, PASSES, 2 * DH], U8, name="qk_scales", align_bytes=64)
+        qk_codes = keep.tile([P, PASSES, BANK], U32, name="qk_codes", align_bytes=64)
+        qk_scales = keep.tile([P, PASSES, BANK], U8, name="qk_scales", align_bytes=64)
         v_codes = keep.tile([P, PASSES, DH], U32, name="v_codes", align_bytes=64)
         v_scales = keep.tile([P, PASSES, DH], U8, name="v_scales", align_bytes=64)
 
@@ -409,12 +422,12 @@ def tile_transformerlayershard_pa_t_kernel(
         def live(n):
             return 0 <= n < TILES
 
-        for k in range(TILES + 2):
+        for k in range(TILES + 3):
             u = k // UNIT
             if k % UNIT == 0 and u + 4 < UNITS and u > 0:
                 load(u + 4)
-            if k % UNIT == 0 and u > 0:
-                project(u - 1)
+            if live(k - 2):
+                project(k - 2)
             if live(k):
                 gain(k)
             if k == 0:
@@ -424,12 +437,12 @@ def tile_transformerlayershard_pa_t_kernel(
                 table_values(0)
             if live(k + 4):
                 row_sum(k + 4)
-            if k % UNIT == 0 and u > 0:
-                rotate(u - 1)
-            if k % UNIT == 1 and u > 0:
-                store_qk(u - 1)
+            if k % UNIT == 0 and u > 1:
+                store_qk(u - 2)
             if k % UNIT == 1 and live(k):
                 quantise(u)
+            if live(k - 2):
+                rotate(k - 2)
             if live(k + 1):
                 turn(k + 1)
             if live(k + 2):
@@ -438,7 +451,7 @@ def tile_transformerlayershard_pa_t_kernel(
                 row_squares(k + 3)
             if live(k + 4):
                 negate_mean(k + 4)
-            if k % UNIT == 0 and u > 0:
+            if k % UNIT == 1 and live(k - 2):
                 store_v(u - 1)
             if k % STEP == 1 and live(k + 3):
                 table_angles((k + 3) // STEP)

@@ -29,7 +29,7 @@ FREQS = DH // 2
 DECADE = FREQS // 4
 ROUND_MAGIC = 12582912.0
 HI_GRID = 2.0 ** 19
-STEP = 4
+STEP = 16
 TINY = 2.0 ** -60
 HEAD_TILES = 4
 VECTOR_SUM_EVERY = 6
@@ -66,7 +66,7 @@ def tile_transformerlayershard_pa_t_kernel(
         v_banks = ctx.enter_context(tc.psum_pool(name="v_banks", bufs=1))
         ctx.enter_context(tc.manual_schedule())
 
-        x_of, sums_of, neg_mean_of, squares_of, y_of = {}, {}, {}, {}, {}
+        x_of, sums_of, neg_mean_of, squares_of, rstd_of, y_of = {}, {}, {}, {}, {}, {}
         turned_of, grouped_of, codes_of, scales_of = {}, {}, {}, {}
         qk_acc_of, v_acc_of, products_of, parts_of = {}, {}, {}, {}
 
@@ -108,21 +108,19 @@ def tile_transformerlayershard_pa_t_kernel(
                 accum_out=squares_of[n][:],
             )
 
+        def row_scale(n):
+            rstd_of[n] = stats.tile([P, 1], F32, tag="rstd", name="rstd")
+            nc.scalar.activation(
+                out=rstd_of[n][:], in_=squares_of[n][:], func=ACT.Abs_reciprocal_sqrt,
+                scale=1.0 / D, bias=eps[:, 0:1],
+            )
+
         def normalise(n):
-            variance = stats.tile([P, 1], F32, tag="variance", name="variance")
-            nc.gpsimd.tensor_scalar(
-                out=variance[:], in0=squares_of[n][:], scalar1=1.0 / D, scalar2=EPS,
-                op0=ALU.mult, op1=ALU.add,
-            )
-            rstd = stats.tile([P, 1], F32, tag="rstd", name="rstd")
-            nc.gpsimd.tensor_tensor(
-                out=rstd[:], in0=variance[:], in1=minus_half[:], op=ALU.pow
-            )
             y_n = work.tile([P, PASSES, PACK, P], F32, tag="y_n", name="y_n")
             engine = nc.vector if n < 2 else nc.gpsimd
             engine.tensor_scalar(
                 out=y_n[:], in0=x_of[n].rearrange("r (h p j) -> r h j p", p=P, j=PACK),
-                scalar1=neg_mean_of[n][:, 0:1], scalar2=rstd[:, 0:1], op0=ALU.add, op1=ALU.mult,
+                scalar1=neg_mean_of[n][:, 0:1], scalar2=rstd_of[n][:, 0:1], op0=ALU.add, op1=ALU.mult,
             )
             y_of[n] = y_n
 
@@ -223,17 +221,17 @@ def tile_transformerlayershard_pa_t_kernel(
 
         def table_angles(g):
             shape = [P, STEP, FREQS]
-            angle = work.tile(shape, F32, tag="angle", name="angle")
+            angle = setup.tile(shape, F32, tag="angle", name="angle", bufs=2)
             nc.vector.scalar_tensor_tensor(
                 out=angle[:], in0=turns[:].unsqueeze(1).to_broadcast(shape),
                 scalar=float(STEP * g), in1=first_angles[:], op0=ALU.mult, op1=ALU.add,
             )
-            whole = work.tile(shape, F32, tag="whole", name="whole")
+            whole = setup.tile(shape, F32, tag="whole", name="whole", bufs=2)
             nc.vector.tensor_scalar(
                 out=whole[:], in0=angle[:], scalar1=ROUND_MAGIC, scalar2=ROUND_MAGIC,
                 op0=ALU.add, op1=ALU.subtract,
             )
-            part = work.tile(shape, F32, tag="part", name="part")
+            part = setup.tile(shape, F32, tag="part", name="part", bufs=2)
             nc.vector.tensor_tensor(out=part[:], in0=angle[:], in1=whole[:], op=ALU.subtract)
             parts_of[g] = part
 
@@ -243,7 +241,7 @@ def tile_transformerlayershard_pa_t_kernel(
                 out=table[:, tiles, 1, :], in_=part[:],
                 func=ACT.Sin, scale=2.0 * math.pi,
             )
-            size = work.tile([P, STEP, FREQS], F32, tag="size", name="size")
+            size = setup.tile([P, STEP, FREQS], F32, tag="size", name="size", bufs=2)
             nc.scalar.activation(out=size[:], in_=part[:], func=ACT.Abs)
             nc.scalar.activation(
                 out=table[:, tiles, 0, :], in_=size[:], func=ACT.Sin, scale=-2.0 * math.pi,
@@ -277,8 +275,8 @@ def tile_transformerlayershard_pa_t_kernel(
         nc.gpsimd.iota(first_i[:], pattern=[[0, 1]], base=0, channel_multiplier=TILES)
         one = setup.tile([P, 1], F32, name="one")
         nc.vector.memset(one[:], 1.0)
-        minus_half = keep.tile([P, 1], F32, name="minus_half")
-        nc.vector.memset(minus_half[:], -0.5)
+        eps = keep.tile([P, 1], F32, name="eps")
+        nc.vector.tensor_scalar(out=eps[:], in0=one[:], scalar1=EPS, scalar2=None, op0=ALU.mult)
         quarter = keep.tile([P, 1], F32, name="quarter")
         nc.vector.tensor_scalar(
             out=quarter[:], in0=one[:], scalar1=math.pi / 2.0, scalar2=None, op0=ALU.mult
@@ -338,53 +336,6 @@ def tile_transformerlayershard_pa_t_kernel(
             nc.scalar.copy(out=offset_rows[:, h, :, :], in_=turned_ratio[:])
         row_squares(1)
 
-        qk_grouped = setup.tile([P, PASSES, BANK, PACK], BF16, name="qk_grouped", align_bytes=64)
-        v_grouped = setup.tile([P, PASSES, DH, PACK], BF16, name="v_grouped", align_bytes=64)
-        for h in range(PASSES):
-            for g in range(2):
-                cols = qk_grouped[:, h, g * 2 * DH : (g + 1) * 2 * DH, :]
-                nc.vector.tensor_copy(
-                    out=cols.rearrange("p (r s c) j -> p r s c j", r=2, s=2)[:, :, 0, :, :],
-                    in_=raws[g][:, h, :, :].rearrange("p j (r c) -> p r c j", r=2),
-                )
-                for a in range(2):
-                    nc.vector.tensor_copy(
-                        out=cols.rearrange("p (r s i e) j -> p r s i e j", r=2, s=2, e=2)[
-                            :, :, 1, :, a, :
-                        ],
-                        in_=raws[g][:, h, :, :].rearrange("p j (r i e) -> p r i e j", r=2, e=2)[
-                            :, :, :, 1 - a, :
-                        ],
-                    )
-        normalise(0)
-        turn(0)
-        row_sum(2)
-        negate_mean(2)
-        row_squares(2)
-        for h in range(PASSES):
-            nc.vector.tensor_copy(
-                out=v_grouped[:, h, :, :], in_=raws[2][:, h, :, :].rearrange("p j n -> p n j")
-            )
-        normalise(1)
-        row_sum(3)
-        negate_mean(3)
-        qk_codes = keep.tile([P, PASSES, BANK], U32, name="qk_codes", align_bytes=64)
-        qk_scales = keep.tile([P, PASSES, BANK], U8, name="qk_scales", align_bytes=64)
-        v_codes = keep.tile([P, PASSES, DH], U32, name="v_codes", align_bytes=64)
-        v_scales = keep.tile([P, PASSES, DH], U8, name="v_scales", align_bytes=64)
-
-        def quantise_weights():
-            nc.vector.quantize_mx(
-                out=qk_codes[:].rearrange("p h n -> p (h n)").bitcast(FP8X4),
-                scales=qk_scales[:].rearrange("p h n -> p (h n)"),
-                in_=qk_grouped[:].rearrange("p h n j -> p (h n j)"),
-            )
-            nc.vector.quantize_mx(
-                out=v_codes[:].rearrange("p h n -> p (h n)").bitcast(FP8X4),
-                scales=v_scales[:].rearrange("p h n -> p (h n)"),
-                in_=v_grouped[:].rearrange("p h n j -> p (h n j)"),
-            )
-
         table = keep.tile([P, TILES, 2, FREQS], F32, name="table")
         first_angles = keep.tile([P, STEP, FREQS], F32, name="first_angles")
 
@@ -412,11 +363,71 @@ def tile_transformerlayershard_pa_t_kernel(
                 out=first_angles[:, 0, 0:DECADE], in0=turns_lo[:], scalar=first[:, 0:1],
                 in1=first_angles[:, 0, 0:DECADE], op0=ALU.mult, op1=ALU.add,
             )
-            for i in range(1, STEP):
+            filled = 1
+            while filled < STEP:
                 nc.vector.scalar_tensor_tensor(
-                    out=first_angles[:, i, :], in0=turns[:], scalar=float(i),
-                    in1=first_angles[:, 0, :], op0=ALU.mult, op1=ALU.add,
+                    out=first_angles[:, filled : 2 * filled, :],
+                    in0=turns[:].unsqueeze(1).to_broadcast([P, filled, FREQS]),
+                    scalar=float(filled), in1=first_angles[:, 0:filled, :],
+                    op0=ALU.mult, op1=ALU.add,
                 )
+                filled *= 2
+
+        start_angles()
+        for g in range(TILES // STEP):
+            table_angles(g)
+            table_values(g)
+            if g == 0:
+                row_sum(2)
+                negate_mean(2)
+            if g == 1:
+                row_sum(3)
+                negate_mean(3)
+
+        qk_grouped = setup.tile([P, PASSES, BANK, PACK], BF16, name="qk_grouped", align_bytes=64)
+        v_grouped = setup.tile([P, PASSES, DH, PACK], BF16, name="v_grouped", align_bytes=64)
+        for h in range(PASSES):
+            for g in range(2):
+                cols = qk_grouped[:, h, g * 2 * DH : (g + 1) * 2 * DH, :]
+                nc.vector.tensor_copy(
+                    out=cols.rearrange("p (r s c) j -> p r s c j", r=2, s=2)[:, :, 0, :, :],
+                    in_=raws[g][:, h, :, :].rearrange("p j (r c) -> p r c j", r=2),
+                )
+                for a in range(2):
+                    nc.vector.tensor_copy(
+                        out=cols.rearrange("p (r s i e) j -> p r s i e j", r=2, s=2, e=2)[
+                            :, :, 1, :, a, :
+                        ],
+                        in_=raws[g][:, h, :, :].rearrange("p j (r i e) -> p r i e j", r=2, e=2)[
+                            :, :, :, 1 - a, :
+                        ],
+                    )
+        row_scale(0)
+        row_scale(1)
+        row_squares(2)
+        normalise(0)
+        turn(0)
+        for h in range(PASSES):
+            nc.vector.tensor_copy(
+                out=v_grouped[:, h, :, :], in_=raws[2][:, h, :, :].rearrange("p j n -> p n j")
+            )
+        normalise(1)
+        qk_codes = keep.tile([P, PASSES, BANK], U32, name="qk_codes", align_bytes=64)
+        qk_scales = keep.tile([P, PASSES, BANK], U8, name="qk_scales", align_bytes=64)
+        v_codes = keep.tile([P, PASSES, DH], U32, name="v_codes", align_bytes=64)
+        v_scales = keep.tile([P, PASSES, DH], U8, name="v_scales", align_bytes=64)
+
+        def quantise_weights():
+            nc.vector.quantize_mx(
+                out=qk_codes[:].rearrange("p h n -> p (h n)").bitcast(FP8X4),
+                scales=qk_scales[:].rearrange("p h n -> p (h n)"),
+                in_=qk_grouped[:].rearrange("p h n j -> p (h n j)"),
+            )
+            nc.vector.quantize_mx(
+                out=v_codes[:].rearrange("p h n -> p (h n)").bitcast(FP8X4),
+                scales=v_scales[:].rearrange("p h n -> p (h n)"),
+                in_=v_grouped[:].rearrange("p h n j -> p (h n j)"),
+            )
 
 
         def live(n):
@@ -432,9 +443,6 @@ def tile_transformerlayershard_pa_t_kernel(
                 gain(k)
             if k == 0:
                 quantise_weights()
-                start_angles()
-                table_angles(0)
-                table_values(0)
             if live(k + 4):
                 row_sum(k + 4)
             if k % UNIT == 0 and u > 1:
@@ -446,6 +454,7 @@ def tile_transformerlayershard_pa_t_kernel(
             if live(k + 1):
                 turn(k + 1)
             if live(k + 2):
+                row_scale(k + 2)
                 normalise(k + 2)
             if live(k + 3):
                 row_squares(k + 3)
@@ -453,7 +462,3 @@ def tile_transformerlayershard_pa_t_kernel(
                 negate_mean(k + 4)
             if k % UNIT == 1 and live(k - 2):
                 store_v(u - 1)
-            if k % STEP == 1 and live(k + 3):
-                table_angles((k + 3) // STEP)
-            if k % STEP == 2 and live(k + 2):
-                table_values((k + 2) // STEP)

@@ -32,8 +32,7 @@ HI_GRID = 2.0 ** 19
 STEP = 16
 TINY = 2.0 ** -60
 HEAD_TILES = 4
-VECTOR_SUM_EVERY = 6
-WARM_COLS = 32
+VECTOR_SUM_EVERY = 5
 X_BUFS = 8
 
 FLOPS = 2 * S * D * 3 * DH
@@ -66,9 +65,10 @@ def tile_transformerlayershard_pa_t_kernel(
         v_banks = ctx.enter_context(tc.psum_pool(name="v_banks", bufs=1))
         ctx.enter_context(tc.manual_schedule())
 
-        x_of, sums_of, neg_mean_of, squares_of, rstd_of, y_of = {}, {}, {}, {}, {}, {}
+        x_of, neg_mean_of, squares_of, rstd_of, y_of = {}, {}, {}, {}, {}
         turned_of, grouped_of, codes_of, scales_of = {}, {}, {}, {}
-        qk_acc_of, v_acc_of, products_of, parts_of = {}, {}, {}, {}
+        qk_acc_of, v_acc_of, products_of = {}, {}, {}
+        angle_of, whole_of, parts_of = {}, {}, {}
 
 
         def load(u):
@@ -81,24 +81,20 @@ def tile_transformerlayershard_pa_t_kernel(
             for t in range(UNIT):
                 x_of[u * UNIT + t] = x_u[:, t, :]
 
-        def row_sum(n):
-            sums_of[n] = stats.tile([P, 1], F32, tag="sums", name="sums")
-            if n < HEAD_TILES or n % VECTOR_SUM_EVERY == 1:
+        def row_mean(n):
+            neg_mean_of[n] = stats.tile([P, 1], F32, tag="neg_mean", name="neg_mean")
+            if n < 2 or n % VECTOR_SUM_EVERY == 4:
                 unread_v = work.tile([P, D], BF16, tag="unread_v", name="unread_v")
                 nc.vector.tensor_scalar(
-                    out=unread_v[:], in0=x_of[n], scalar1=1.0, scalar2=None,
-                    op0=ALU.mult, op1=ALU.add, accum_out=sums_of[n][:],
+                    out=unread_v[:], in0=x_of[n], scalar1=-1.0 / D, scalar2=None,
+                    op0=ALU.mult, op1=ALU.add, accum_out=neg_mean_of[n][:],
                 )
             else:
                 unread_s = work.tile([P, D], BF16, tag="unread_s", name="unread_s")
                 nc.scalar.activation(
-                    out=unread_s[:], in_=x_of[n], func=ACT.Copy, scale=1.0, accum_out=sums_of[n][:]
+                    out=unread_s[:], in_=x_of[n], func=ACT.Copy, scale=-1.0 / D,
+                    accum_out=neg_mean_of[n][:],
                 )
-
-        def negate_mean(n):
-            neg_mean = stats.tile([P, 1], F32, tag="neg_mean", name="neg_mean")
-            nc.scalar.activation(out=neg_mean[:], in_=sums_of[n][:], func=ACT.Copy, scale=-1.0 / D)
-            neg_mean_of[n] = neg_mean
 
         def row_squares(n):
             squares_of[n] = stats.tile([P, 1], F32, tag="squares", name="squares")
@@ -127,19 +123,21 @@ def tile_transformerlayershard_pa_t_kernel(
         def turn(n):
             for h in range(PASSES):
                 turned = turned_banks.tile([P, PACK, P], F32, tag="turned", name="turned")
-                nc.tensor.matmul(
-                    turned[:, 0, 0:WARM_COLS], lhsT=ident[:], rhs=ident[:, 0:WARM_COLS],
-                    start=True, stop=True,
-                )
                 for j in range(PACK):
                     nc.tensor.matmul(
                         turned[:, j, :], lhsT=y_of[n][:, h, j, :], rhs=ident[:],
                         is_transpose=True, start=True, stop=False,
                     )
-                    nc.tensor.matmul(
-                        turned[:, j, :], lhsT=offset_rows[:, h, j, :], rhs=ident[:],
-                        is_transpose=True, start=False, stop=True,
-                    )
+                    if j == PACK - 1 and n >= HEAD_TILES:
+                        nc.tensor.matmul(
+                            turned[:, j, :], lhsT=offset_parts[:, h, :], rhs=ones[:],
+                            start=False, stop=True,
+                        )
+                    else:
+                        nc.tensor.matmul(
+                            turned[:, j, :], lhsT=offset_rows[:, h, j, :], rhs=ident[:],
+                            is_transpose=True, start=False, stop=True,
+                        )
                 turned_of[(n, h)] = turned
 
         def gain(n):
@@ -172,15 +170,15 @@ def tile_transformerlayershard_pa_t_kernel(
         def project(n):
             u, t = n // UNIT, n % UNIT
             codes, scales = codes_of[u], scales_of[u]
-            qk_acc = qk_banks.tile([P, BANK], F32, tag="qk_acc", name="qk_acc")
             if t == 0:
+                qk_acc_of[u] = qk_banks.tile([P, UNIT, 2 * DH], F32, tag="qk_acc", name="qk_acc")
                 v_acc_of[u] = v_banks.tile([P, UNIT, DH], F32, tag="v_acc", name="v_acc")
             for acc, w_codes, w_scales in (
-                (qk_acc[:], qk_codes, qk_scales), (v_acc_of[u][:, t, :], v_codes, v_scales)
+                (qk_acc_of[u], qk_codes, qk_scales), (v_acc_of[u], v_codes, v_scales)
             ):
                 for h in range(PASSES):
                     nc.tensor.matmul_mx(
-                        out=acc,
+                        out=acc[:, t, :],
                         lhsT=codes[:, t, h, :].bitcast(FP8X4),
                         lhsT_scale=scales[:, t, h, :],
                         rhs=w_codes[:, h, :].bitcast(FP8X4),
@@ -188,57 +186,65 @@ def tile_transformerlayershard_pa_t_kernel(
                         start=(h == 0),
                         stop=(h == PASSES - 1),
                     )
-            qk_acc_of[n] = qk_acc
 
-        def rotate(n):
-            u, t = n // UNIT, n % UNIT
-            if t == 0:
-                products_of[u] = work.tile([P, UNIT, 4, DH], F32, tag="products", name="products")
+        def rotate(u):
+            tiles = slice(u * UNIT, (u + 1) * UNIT)
+            shape = [P, UNIT, 2, 4, FREQS]
+            products = work.tile([P, UNIT, 2, 2 * DH], F32, tag="products", name="products")
             nc.vector.tensor_tensor(
-                out=products_of[u][:, t, :, :],
-                in0=qk_acc_of[n][:].rearrange("p (a w) -> p a w", a=4),
-                in1=table[:, n, :, :].rearrange("p s c -> p (s c)").unsqueeze(1)
-                .to_broadcast([P, 4, DH]),
+                out=products[:].rearrange("p t s (g c) -> p t s g c", c=FREQS),
+                in0=qk_acc_of[u][:].rearrange("p t (g c) -> p t g c", c=FREQS)
+                .unsqueeze(2).to_broadcast(shape),
+                in1=table[:, tiles, :, :].unsqueeze(3).to_broadcast(shape),
                 op=ALU.mult,
             )
+            products_of[u] = products
 
         def store_qk(u):
             tiles, products = slice(u * UNIT, (u + 1) * UNIT), products_of[u]
-            qk_out = work.tile([P, UNIT, 2, DH], F32, tag="qk_out", name="qk_out")
+            qk_out = work.tile([P, 2, UNIT, DH], F32, tag="qk_out", name="qk_out")
             nc.vector.tensor_tensor(
-                out=qk_out[:].rearrange("p t g (r c) -> p (t g r) c", r=2),
-                in0=products[:, :, :, 0:FREQS].rearrange("p t a c -> p (t a) c"),
-                in1=products[:, :, :, FREQS:DH].rearrange("p t a c -> p (t a) c"),
+                out=qk_out[:].rearrange("p g t (i e) -> p t g i e", e=2),
+                in0=products[:, :, 0, :].rearrange("p t (g i e) -> p t g i e", g=2, e=2),
+                in1=products[:, :, 1, :].rearrange("p t (g i e) -> p t g i e", g=2, e=2)[
+                    :, :, :, :, ::-1
+                ],
                 op=ALU.add,
             )
-            nc.sync.dma_start(out=q_rows[:, tiles, :], in_=qk_out[:, :, 0, :])
-            nc.sync.dma_start(out=k_rows[:, tiles, :], in_=qk_out[:, :, 1, :])
+            nc.sync.dma_start(out=q_rows[:, tiles, :], in_=qk_out[:, 0, :, :])
+            nc.sync.dma_start(out=k_rows[:, tiles, :], in_=qk_out[:, 1, :, :])
 
         def store_v(u):
             v_out = work.tile([P, UNIT, DH], F32, tag="v_out", name="v_out")
             nc.scalar.copy(out=v_out[:], in_=v_acc_of[u][:])
             nc.sync.dma_start(out=v_rows[:, u * UNIT : (u + 1) * UNIT, :], in_=v_out[:])
 
-        def table_angles(g):
+        def table_turns(g):
             shape = [P, STEP, FREQS]
-            angle = setup.tile(shape, F32, tag="angle", name="angle", bufs=2)
+            angle_of[g] = setup.tile(shape, F32, tag="angle", name="angle", bufs=2)
             nc.vector.scalar_tensor_tensor(
-                out=angle[:], in0=turns[:].unsqueeze(1).to_broadcast(shape),
+                out=angle_of[g][:], in0=turns[:].unsqueeze(1).to_broadcast(shape),
                 scalar=float(STEP * g), in1=first_angles[:], op0=ALU.mult, op1=ALU.add,
             )
-            whole = setup.tile(shape, F32, tag="whole", name="whole", bufs=2)
+
+        def table_wholes(g):
+            whole_of[g] = setup.tile([P, STEP, FREQS], F32, tag="whole", name="whole", bufs=2)
             nc.vector.tensor_scalar(
-                out=whole[:], in0=angle[:], scalar1=ROUND_MAGIC, scalar2=ROUND_MAGIC,
+                out=whole_of[g][:], in0=angle_of[g][:], scalar1=ROUND_MAGIC, scalar2=ROUND_MAGIC,
                 op0=ALU.add, op1=ALU.subtract,
             )
-            part = setup.tile(shape, F32, tag="part", name="part", bufs=2)
-            nc.vector.tensor_tensor(out=part[:], in0=angle[:], in1=whole[:], op=ALU.subtract)
-            parts_of[g] = part
+
+        def table_parts(g):
+            parts_of[g] = setup.tile([P, STEP, FREQS], F32, tag="part", name="part", bufs=2)
+            nc.vector.tensor_tensor(
+                out=parts_of[g][:], in0=angle_of[g][:], in1=whole_of[g][:], op=ALU.subtract
+            )
 
         def table_values(g):
             tiles, part = slice(g * STEP, (g + 1) * STEP), parts_of[g]
             nc.scalar.activation(
-                out=table[:, tiles, 1, :], in_=part[:],
+                out=table[:, tiles, 1, :].rearrange("p t (i e) -> p t i e", e=2),
+                in_=part[:].rearrange("p t (i e) -> p t i e", e=2)[:, :, :, ::-1],
                 func=ACT.Sin, scale=2.0 * math.pi,
             )
             size = setup.tile([P, STEP, FREQS], F32, tag="size", name="size", bufs=2)
@@ -275,12 +281,6 @@ def tile_transformerlayershard_pa_t_kernel(
         nc.gpsimd.iota(first_i[:], pattern=[[0, 1]], base=0, channel_multiplier=TILES)
         one = setup.tile([P, 1], F32, name="one")
         nc.vector.memset(one[:], 1.0)
-        eps = keep.tile([P, 1], F32, name="eps")
-        nc.vector.tensor_scalar(out=eps[:], in0=one[:], scalar1=EPS, scalar2=None, op0=ALU.mult)
-        quarter = keep.tile([P, 1], F32, name="quarter")
-        nc.vector.tensor_scalar(
-            out=quarter[:], in0=one[:], scalar1=math.pi / 2.0, scalar2=None, op0=ALU.mult
-        )
         turns_hi = setup.tile([P, DECADE], F32, name="turns_hi")
         turns_lo = setup.tile([P, DECADE], F32, name="turns_lo")
         for c in range(DECADE):
@@ -298,124 +298,88 @@ def tile_transformerlayershard_pa_t_kernel(
                 out=turns[:, d * DECADE : (d + 1) * DECADE], in0=turns[:, 0:DECADE],
                 scalar1=10.0 ** -d, scalar2=0.0, op0=ALU.mult, op1=ALU.add,
             )
+        eps = keep.tile([P, 1], F32, name="eps")
+        nc.vector.tensor_scalar(out=eps[:], in0=one[:], scalar1=EPS, scalar2=None, op0=ALU.mult)
+        quarter = keep.tile([P, 1], F32, name="quarter")
+        nc.vector.tensor_scalar(
+            out=quarter[:], in0=one[:], scalar1=math.pi / 2.0, scalar2=None, op0=ALU.mult
+        )
+        ones = keep.tile([P, P], BF16, name="ones")
+        nc.vector.memset(ones[:], 1.0)
 
         gains = keep.tile([P, PASSES, PACK], F32, name="gains")
         small = setup.tile([P, PASSES, PACK], F32, name="small")
-        nc.vector.tensor_tensor(
-            out=small[:], in0=scale_cols[:], in1=scale_cols[:], op=ALU.mult
+        ratio = setup.tile([P, PASSES, PACK], F32, name="ratio")
+        first = setup.tile([P, 1], F32, name="first")
+        start = setup.tile([P, FREQS], F32, name="start")
+        start_whole = setup.tile([P, FREQS], F32, name="start_whole")
+        first_angles = keep.tile([P, STEP, FREQS], F32, name="first_angles")
+        nc.vector.tensor_copy(out=first[:], in_=first_i[:])
+        nc.vector.tensor_tensor(out=small[:], in0=scale_cols[:], in1=scale_cols[:], op=ALU.mult)
+        nc.vector.tensor_scalar(
+            out=start[:, 0:DECADE], in0=turns_hi[:], scalar1=first[:, 0:1], scalar2=None,
+            op0=ALU.mult,
         )
-        row_sum(0)
-        negate_mean(0)
+        nc.vector.tensor_scalar(
+            out=start[:, DECADE:FREQS], in0=turns[:, DECADE:FREQS], scalar1=first[:, 0:1],
+            scalar2=None, op0=ALU.mult,
+        )
         nc.vector.tensor_scalar(
             out=small[:], in0=small[:], scalar1=TINY * TINY, scalar2=TINY,
             op0=ALU.is_lt, op1=ALU.mult,
         )
-        row_squares(0)
-        nc.vector.tensor_tensor(
-            out=gains[:], in0=scale_cols[:], in1=small[:], op=ALU.add
+        nc.vector.tensor_scalar(
+            out=start_whole[:], in0=start[:], scalar1=ROUND_MAGIC, scalar2=ROUND_MAGIC,
+            op0=ALU.add, op1=ALU.subtract,
         )
-        row_sum(1)
-        negate_mean(1)
-        ratio = setup.tile([P, PASSES, PACK], F32, name="ratio")
+        nc.vector.tensor_tensor(out=gains[:], in0=scale_cols[:], in1=small[:], op=ALU.add)
+        nc.vector.tensor_tensor(
+            out=first_angles[:, 0, :], in0=start[:], in1=start_whole[:], op=ALU.subtract
+        )
         nc.vector.reciprocal(out=ratio[:], in_=gains[:])
-        nc.vector.tensor_tensor(
-            out=ratio[:], in0=ratio[:], in1=offset_cols[:], op=ALU.mult
+        nc.vector.scalar_tensor_tensor(
+            out=first_angles[:, 0, 0:DECADE], in0=turns_lo[:], scalar=first[:, 0:1],
+            in1=first_angles[:, 0, 0:DECADE], op0=ALU.mult, op1=ALU.add,
         )
+        nc.vector.tensor_tensor(out=ratio[:], in0=ratio[:], in1=offset_cols[:], op=ALU.mult)
+
+        def more_first_angles(filled):
+            nc.vector.scalar_tensor_tensor(
+                out=first_angles[:, filled : 2 * filled, :],
+                in0=turns[:].unsqueeze(1).to_broadcast([P, filled, FREQS]),
+                scalar=float(filled), in1=first_angles[:, 0:filled, :],
+                op0=ALU.mult, op1=ALU.add,
+            )
+
+        more_first_angles(1)
+        row_mean(0)
+        more_first_angles(2)
         ratio_cols = setup.tile([P, SLOTS, P], F32, name="ratio_cols")
         nc.vector.tensor_copy(
             out=ratio_cols[:],
             in_=ratio[:].rearrange("p h j -> p (h j)").unsqueeze(2).to_broadcast([P, SLOTS, P]),
         )
-        offset_rows = keep.tile([P, PASSES, PACK, P], F32, name="offset_rows")
-        for h in range(PASSES):
-            turned_ratio = turned_banks.tile([P, PACK, P], F32, tag="turned", name="turned_ratio")
-            for j in range(PACK):
-                nc.tensor.transpose(
-                    turned_ratio[:, j, :], ratio_cols[:, h * PACK + j, :], ident[:]
-                )
-            nc.scalar.copy(out=offset_rows[:, h, :, :], in_=turned_ratio[:])
+        more_first_angles(4)
+        row_mean(1)
+        more_first_angles(8)
+        row_squares(0)
         row_squares(1)
-
+        row_mean(2)
         table = keep.tile([P, TILES, 2, FREQS], F32, name="table")
-        first_angles = keep.tile([P, STEP, FREQS], F32, name="first_angles")
 
-        def start_angles():
-            first = setup.tile([P, 1], F32, name="first")
-            nc.vector.tensor_copy(out=first[:], in_=first_i[:])
-            start = setup.tile([P, FREQS], F32, name="start")
-            nc.vector.tensor_scalar(
-                out=start[:, 0:DECADE], in0=turns_hi[:], scalar1=first[:, 0:1], scalar2=None,
-                op0=ALU.mult,
-            )
-            nc.vector.tensor_scalar(
-                out=start[:, DECADE:FREQS], in0=turns[:, DECADE:FREQS], scalar1=first[:, 0:1],
-                scalar2=None, op0=ALU.mult,
-            )
-            start_whole = setup.tile([P, FREQS], F32, name="start_whole")
-            nc.vector.tensor_scalar(
-                out=start_whole[:], in0=start[:], scalar1=ROUND_MAGIC, scalar2=ROUND_MAGIC,
-                op0=ALU.add, op1=ALU.subtract,
-            )
-            nc.vector.tensor_tensor(
-                out=first_angles[:, 0, :], in0=start[:], in1=start_whole[:], op=ALU.subtract
-            )
-            nc.vector.scalar_tensor_tensor(
-                out=first_angles[:, 0, 0:DECADE], in0=turns_lo[:], scalar=first[:, 0:1],
-                in1=first_angles[:, 0, 0:DECADE], op0=ALU.mult, op1=ALU.add,
-            )
-            filled = 1
-            while filled < STEP:
-                nc.vector.scalar_tensor_tensor(
-                    out=first_angles[:, filled : 2 * filled, :],
-                    in0=turns[:].unsqueeze(1).to_broadcast([P, filled, FREQS]),
-                    scalar=float(filled), in1=first_angles[:, 0:filled, :],
-                    op0=ALU.mult, op1=ALU.add,
-                )
-                filled *= 2
-
-        start_angles()
-        for g in range(TILES // STEP):
-            table_angles(g)
-            table_values(g)
-            if g == 0:
-                row_sum(2)
-                negate_mean(2)
-            if g == 1:
-                row_sum(3)
-                negate_mean(3)
-
-        qk_grouped = setup.tile([P, PASSES, BANK, PACK], BF16, name="qk_grouped", align_bytes=64)
+        qk_grouped = setup.tile([P, PASSES, 2 * DH, PACK], BF16, name="qk_grouped", align_bytes=64)
         v_grouped = setup.tile([P, PASSES, DH, PACK], BF16, name="v_grouped", align_bytes=64)
-        for h in range(PASSES):
-            for g in range(2):
-                cols = qk_grouped[:, h, g * 2 * DH : (g + 1) * 2 * DH, :]
-                nc.vector.tensor_copy(
-                    out=cols.rearrange("p (r s c) j -> p r s c j", r=2, s=2)[:, :, 0, :, :],
-                    in_=raws[g][:, h, :, :].rearrange("p j (r c) -> p r c j", r=2),
-                )
-                for a in range(2):
-                    nc.vector.tensor_copy(
-                        out=cols.rearrange("p (r s i e) j -> p r s i e j", r=2, s=2, e=2)[
-                            :, :, 1, :, a, :
-                        ],
-                        in_=raws[g][:, h, :, :].rearrange("p j (r i e) -> p r i e j", r=2, e=2)[
-                            :, :, :, 1 - a, :
-                        ],
-                    )
-        row_scale(0)
-        row_scale(1)
-        row_squares(2)
-        normalise(0)
-        turn(0)
-        for h in range(PASSES):
-            nc.vector.tensor_copy(
-                out=v_grouped[:, h, :, :], in_=raws[2][:, h, :, :].rearrange("p j n -> p n j")
-            )
-        normalise(1)
-        qk_codes = keep.tile([P, PASSES, BANK], U32, name="qk_codes", align_bytes=64)
-        qk_scales = keep.tile([P, PASSES, BANK], U8, name="qk_scales", align_bytes=64)
+        qk_codes = keep.tile([P, PASSES, 2 * DH], U32, name="qk_codes", align_bytes=64)
+        qk_scales = keep.tile([P, PASSES, 2 * DH], U8, name="qk_scales", align_bytes=64)
         v_codes = keep.tile([P, PASSES, DH], U32, name="v_codes", align_bytes=64)
         v_scales = keep.tile([P, PASSES, DH], U8, name="v_scales", align_bytes=64)
+
+        def group_weights(g):
+            for h in range(PASSES):
+                out = v_grouped[:, h, :, :]
+                if g < 2:
+                    out = qk_grouped[:, h, g * DH : (g + 1) * DH, :]
+                nc.vector.tensor_copy(out=out, in_=raws[g][:, h, :, :].rearrange("p j n -> p n j"))
 
         def quantise_weights():
             nc.vector.quantize_mx(
@@ -429,11 +393,68 @@ def tile_transformerlayershard_pa_t_kernel(
                 in_=v_grouped[:].rearrange("p h n j -> p (h n j)"),
             )
 
+        offset_rows = keep.tile([P, PASSES, PACK, P], F32, name="offset_rows")
+        for h in range(PASSES):
+            turned_ratio = turned_banks.tile([P, PACK, P], F32, tag="turned", name="turned_ratio")
+            for j in range(PACK):
+                nc.tensor.transpose(
+                    turned_ratio[:, j, :], ratio_cols[:, h * PACK + j, :], ident[:]
+                )
+            nc.scalar.copy(out=offset_rows[:, h, :, :], in_=turned_ratio[:])
+
+        offset_parts = keep.tile([P, PASSES, P], BF16, name="offset_parts")
+        rest = setup.tile([P, PASSES, P], F32, name="rest")
+        nc.gpsimd.tensor_scalar(
+            out=rest[:], in0=offset_rows[:, :, PACK - 1, :], scalar1=1.0, scalar2=0.0,
+            op0=ALU.mult, op1=ALU.add,
+        )
+        total = setup.tile([P, PASSES, P], F32, name="total")
+        for i in range(3):
+            here = setup.tile([P, 1], F32, tag="here", name="here", bufs=3)
+            nc.vector.tensor_scalar(
+                out=here[:], in0=first[:], scalar1=float(TILES * i), scalar2=None, op0=ALU.is_equal
+            )
+            part = setup.tile([P, PASSES, P], BF16, tag="offset_part", name="part", bufs=3)
+            nc.gpsimd.tensor_scalar(
+                out=part[:], in0=rest[:], scalar1=1.0, scalar2=0.0, op0=ALU.mult, op1=ALU.add
+            )
+            if i < 2:
+                nc.gpsimd.tensor_tensor(out=rest[:], in0=rest[:], in1=part[:], op=ALU.subtract)
+            chosen = total
+            if i > 0:
+                chosen = setup.tile([P, PASSES, P], F32, tag="chosen", name="chosen", bufs=2)
+            nc.gpsimd.tensor_scalar(
+                out=chosen[:], in0=part[:], scalar1=here[:, 0:1], scalar2=0.0,
+                op0=ALU.mult, op1=ALU.add,
+            )
+            if i > 0:
+                nc.gpsimd.tensor_tensor(out=total[:], in0=total[:], in1=chosen[:], op=ALU.add)
+        nc.gpsimd.tensor_scalar(
+            out=offset_parts[:], in0=total[:], scalar1=1.0, scalar2=0.0, op0=ALU.mult, op1=ALU.add
+        )
+
+        for g in range(TILES // STEP):
+            table_turns(g)
+            if g < 3:
+                group_weights(g)
+            table_wholes(g)
+            if g == 3:
+                quantise_weights()
+            table_parts(g)
+            table_values(g)
+        row_mean(3)
+        row_scale(0)
+        row_scale(1)
+        row_squares(2)
+        normalise(0)
+        turn(0)
+        normalise(1)
+
 
         def live(n):
             return 0 <= n < TILES
 
-        for k in range(TILES + 3):
+        for k in range(TILES + 4):
             u = k // UNIT
             if k % UNIT == 0 and u + 4 < UNITS and u > 0:
                 load(u + 4)
@@ -441,16 +462,14 @@ def tile_transformerlayershard_pa_t_kernel(
                 project(k - 2)
             if live(k):
                 gain(k)
-            if k == 0:
-                quantise_weights()
             if live(k + 4):
-                row_sum(k + 4)
+                row_mean(k + 4)
             if k % UNIT == 0 and u > 1:
                 store_qk(u - 2)
+            if k % UNIT == 1 and live(k - 2):
+                rotate(u - 1)
             if k % UNIT == 1 and live(k):
                 quantise(u)
-            if live(k - 2):
-                rotate(k - 2)
             if live(k + 1):
                 turn(k + 1)
             if live(k + 2):
@@ -458,7 +477,5 @@ def tile_transformerlayershard_pa_t_kernel(
                 normalise(k + 2)
             if live(k + 3):
                 row_squares(k + 3)
-            if live(k + 4):
-                negate_mean(k + 4)
             if k % UNIT == 1 and live(k - 2):
                 store_v(u - 1)

@@ -33,6 +33,7 @@ STEP = 16
 TINY = 2.0 ** -60
 HEAD_TILES = 4
 VECTOR_SUM_EVERY = 5
+WARM_COLS = 24
 X_BUFS = 8
 
 FLOPS = 2 * S * D * 3 * DH
@@ -123,6 +124,10 @@ def tile_transformerlayershard_pa_t_kernel(
         def turn(n):
             for h in range(PASSES):
                 turned = turned_banks.tile([P, PACK, P], F32, tag="turned", name="turned")
+                nc.tensor.matmul(
+                    turned[:, 0, 0:WARM_COLS], lhsT=ident[:], rhs=ident[:, 0:WARM_COLS],
+                    start=True, stop=True,
+                )
                 for j in range(PACK):
                     nc.tensor.matmul(
                         turned[:, j, :], lhsT=y_of[n][:, h, j, :], rhs=ident[:],
@@ -170,15 +175,15 @@ def tile_transformerlayershard_pa_t_kernel(
         def project(n):
             u, t = n // UNIT, n % UNIT
             codes, scales = codes_of[u], scales_of[u]
+            qk_acc = qk_banks.tile([P, BANK], F32, tag="qk_acc", name="qk_acc")
             if t == 0:
-                qk_acc_of[u] = qk_banks.tile([P, UNIT, 2 * DH], F32, tag="qk_acc", name="qk_acc")
                 v_acc_of[u] = v_banks.tile([P, UNIT, DH], F32, tag="v_acc", name="v_acc")
             for acc, w_codes, w_scales in (
-                (qk_acc_of[u], qk_codes, qk_scales), (v_acc_of[u], v_codes, v_scales)
+                (qk_acc[:], qk_codes, qk_scales), (v_acc_of[u][:, t, :], v_codes, v_scales)
             ):
                 for h in range(PASSES):
                     nc.tensor.matmul_mx(
-                        out=acc[:, t, :],
+                        out=acc,
                         lhsT=codes[:, t, h, :].bitcast(FP8X4),
                         lhsT_scale=scales[:, t, h, :],
                         rhs=w_codes[:, h, :].bitcast(FP8X4),
@@ -186,33 +191,31 @@ def tile_transformerlayershard_pa_t_kernel(
                         start=(h == 0),
                         stop=(h == PASSES - 1),
                     )
+            qk_acc_of[n] = qk_acc
 
-        def rotate(u):
-            tiles = slice(u * UNIT, (u + 1) * UNIT)
-            shape = [P, UNIT, 2, 4, FREQS]
-            products = work.tile([P, UNIT, 2, 2 * DH], F32, tag="products", name="products")
+        def rotate(n):
+            u, t = n // UNIT, n % UNIT
+            if t == 0:
+                products_of[u] = work.tile([P, UNIT, 4, DH], F32, tag="products", name="products")
             nc.vector.tensor_tensor(
-                out=products[:].rearrange("p t s (g c) -> p t s g c", c=FREQS),
-                in0=qk_acc_of[u][:].rearrange("p t (g c) -> p t g c", c=FREQS)
-                .unsqueeze(2).to_broadcast(shape),
-                in1=table[:, tiles, :, :].unsqueeze(3).to_broadcast(shape),
+                out=products_of[u][:, t, :, :],
+                in0=qk_acc_of[n][:].rearrange("p (a w) -> p a w", a=4),
+                in1=table[:, n, :, :].rearrange("p s c -> p (s c)").unsqueeze(1)
+                .to_broadcast([P, 4, DH]),
                 op=ALU.mult,
             )
-            products_of[u] = products
 
         def store_qk(u):
             tiles, products = slice(u * UNIT, (u + 1) * UNIT), products_of[u]
-            qk_out = work.tile([P, 2, UNIT, DH], F32, tag="qk_out", name="qk_out")
+            qk_out = work.tile([P, UNIT, 2, DH], F32, tag="qk_out", name="qk_out")
             nc.vector.tensor_tensor(
-                out=qk_out[:].rearrange("p g t (i e) -> p t g i e", e=2),
-                in0=products[:, :, 0, :].rearrange("p t (g i e) -> p t g i e", g=2, e=2),
-                in1=products[:, :, 1, :].rearrange("p t (g i e) -> p t g i e", g=2, e=2)[
-                    :, :, :, :, ::-1
-                ],
+                out=qk_out[:].rearrange("p t g (r c) -> p (t g r) c", r=2),
+                in0=products[:, :, :, 0:FREQS].rearrange("p t a c -> p (t a) c"),
+                in1=products[:, :, :, FREQS:DH].rearrange("p t a c -> p (t a) c"),
                 op=ALU.add,
             )
-            nc.sync.dma_start(out=q_rows[:, tiles, :], in_=qk_out[:, 0, :, :])
-            nc.sync.dma_start(out=k_rows[:, tiles, :], in_=qk_out[:, 1, :, :])
+            nc.sync.dma_start(out=q_rows[:, tiles, :], in_=qk_out[:, :, 0, :])
+            nc.sync.dma_start(out=k_rows[:, tiles, :], in_=qk_out[:, :, 1, :])
 
         def store_v(u):
             v_out = work.tile([P, UNIT, DH], F32, tag="v_out", name="v_out")
@@ -243,9 +246,7 @@ def tile_transformerlayershard_pa_t_kernel(
         def table_values(g):
             tiles, part = slice(g * STEP, (g + 1) * STEP), parts_of[g]
             nc.scalar.activation(
-                out=table[:, tiles, 1, :].rearrange("p t (i e) -> p t i e", e=2),
-                in_=part[:].rearrange("p t (i e) -> p t i e", e=2)[:, :, :, ::-1],
-                func=ACT.Sin, scale=2.0 * math.pi,
+                out=table[:, tiles, 1, :], in_=part[:], func=ACT.Sin, scale=2.0 * math.pi,
             )
             size = setup.tile([P, STEP, FREQS], F32, tag="size", name="size", bufs=2)
             nc.scalar.activation(out=size[:], in_=part[:], func=ACT.Abs)
@@ -367,19 +368,35 @@ def tile_transformerlayershard_pa_t_kernel(
         row_mean(2)
         table = keep.tile([P, TILES, 2, FREQS], F32, name="table")
 
-        qk_grouped = setup.tile([P, PASSES, 2 * DH, PACK], BF16, name="qk_grouped", align_bytes=64)
+        qk_grouped = setup.tile([P, PASSES, BANK, PACK], BF16, name="qk_grouped", align_bytes=64)
         v_grouped = setup.tile([P, PASSES, DH, PACK], BF16, name="v_grouped", align_bytes=64)
-        qk_codes = keep.tile([P, PASSES, 2 * DH], U32, name="qk_codes", align_bytes=64)
-        qk_scales = keep.tile([P, PASSES, 2 * DH], U8, name="qk_scales", align_bytes=64)
+        qk_codes = keep.tile([P, PASSES, BANK], U32, name="qk_codes", align_bytes=64)
+        qk_scales = keep.tile([P, PASSES, BANK], U8, name="qk_scales", align_bytes=64)
         v_codes = keep.tile([P, PASSES, DH], U32, name="v_codes", align_bytes=64)
         v_scales = keep.tile([P, PASSES, DH], U8, name="v_scales", align_bytes=64)
 
         def group_weights(g):
             for h in range(PASSES):
-                out = v_grouped[:, h, :, :]
-                if g < 2:
-                    out = qk_grouped[:, h, g * DH : (g + 1) * DH, :]
-                nc.vector.tensor_copy(out=out, in_=raws[g][:, h, :, :].rearrange("p j n -> p n j"))
+                rows = raws[g][:, h, :, :]
+                if g == 2:
+                    nc.vector.tensor_copy(
+                        out=v_grouped[:, h, :, :], in_=rows.rearrange("p j n -> p n j")
+                    )
+                    continue
+                cols = qk_grouped[:, h, g * 2 * DH : (g + 1) * 2 * DH, :]
+                nc.vector.tensor_copy(
+                    out=cols.rearrange("p (r s c) j -> p r s c j", r=2, s=2)[:, :, 0, :, :],
+                    in_=rows.rearrange("p j (r c) -> p r c j", r=2),
+                )
+                for a in range(2):
+                    nc.vector.tensor_copy(
+                        out=cols.rearrange("p (r s i e) j -> p r s i e j", r=2, s=2, e=2)[
+                            :, :, 1, :, a, :
+                        ],
+                        in_=rows.rearrange("p j (r i e) -> p r i e j", r=2, e=2)[
+                            :, :, :, 1 - a, :
+                        ],
+                    )
 
         def quantise_weights():
             nc.vector.quantize_mx(
@@ -466,8 +483,8 @@ def tile_transformerlayershard_pa_t_kernel(
                 row_mean(k + 4)
             if k % UNIT == 0 and u > 1:
                 store_qk(u - 2)
-            if k % UNIT == 1 and live(k - 2):
-                rotate(u - 1)
+            if live(k - 2):
+                rotate(k - 2)
             if k % UNIT == 1 and live(k):
                 quantise(u)
             if live(k + 1):

@@ -20,7 +20,6 @@ DH = 128
 EPS = 1e-5
 PACK = 4
 PASSES = D // (P * PACK)
-SLOTS = PASSES * PACK
 TILES = S // P
 UNIT = 2
 UNITS = TILES // UNIT
@@ -29,11 +28,9 @@ FREQS = DH // 2
 DECADE = FREQS // 4
 ROUND_MAGIC = 12582912.0
 HI_GRID = 2.0 ** 19
-STEP = 16
+STEP = 8
 TINY = 2.0 ** -60
-HEAD_TILES = 4
-VECTOR_SUM_EVERY = 5
-WARM_COLS = 24
+HEAD_TILES = 2
 X_BUFS = 8
 
 FLOPS = 2 * S * D * 3 * DH
@@ -61,13 +58,15 @@ def tile_transformerlayershard_pa_t_kernel(
         loads = ctx.enter_context(tc.tile_pool(name="loads", bufs=X_BUFS))
         stats = ctx.enter_context(tc.tile_pool(name="stats", bufs=8))
         work = ctx.enter_context(tc.tile_pool(name="work", bufs=3))
-        turned_banks = ctx.enter_context(tc.psum_pool(name="turned_banks", bufs=5))
+        turned_banks = ctx.enter_context(tc.psum_pool(name="turned_banks", bufs=2))
+        pair_banks = ctx.enter_context(tc.psum_pool(name="pair_banks", bufs=3))
         qk_banks = ctx.enter_context(tc.psum_pool(name="qk_banks", bufs=2))
         v_banks = ctx.enter_context(tc.psum_pool(name="v_banks", bufs=1))
         ctx.enter_context(tc.manual_schedule())
 
         x_of, neg_mean_of, squares_of, rstd_of, y_of = {}, {}, {}, {}, {}
-        turned_of, grouped_of, codes_of, scales_of = {}, {}, {}, {}
+        turned_of, pairs_of, planes_of = {}, {}, {}
+        grouped_of, codes_of, scales_of = {}, {}, {}
         qk_acc_of, v_acc_of, products_of = {}, {}, {}
         angle_of, whole_of, parts_of = {}, {}, {}
 
@@ -84,7 +83,7 @@ def tile_transformerlayershard_pa_t_kernel(
 
         def row_mean(n):
             neg_mean_of[n] = stats.tile([P, 1], F32, tag="neg_mean", name="neg_mean")
-            if n < 2 or n % VECTOR_SUM_EVERY == 4:
+            if n < HEAD_TILES or n % 2 == 1 or n % 8 == 4:
                 unread_v = work.tile([P, D], BF16, tag="unread_v", name="unread_v")
                 nc.vector.tensor_scalar(
                     out=unread_v[:], in0=x_of[n], scalar1=-1.0 / D, scalar2=None,
@@ -114,7 +113,7 @@ def tile_transformerlayershard_pa_t_kernel(
 
         def normalise(n):
             y_n = work.tile([P, PASSES, PACK, P], F32, tag="y_n", name="y_n")
-            engine = nc.vector if n < 2 else nc.gpsimd
+            engine = nc.vector if n < HEAD_TILES else nc.gpsimd
             engine.tensor_scalar(
                 out=y_n[:], in0=x_of[n].rearrange("r (h p j) -> r h j p", p=P, j=PACK),
                 scalar1=neg_mean_of[n][:, 0:1], scalar2=rstd_of[n][:, 0:1], op0=ALU.add, op1=ALU.mult,
@@ -122,52 +121,64 @@ def tile_transformerlayershard_pa_t_kernel(
             y_of[n] = y_n
 
         def turn(n):
-            for h in range(PASSES):
-                turned = turned_banks.tile([P, PACK, P], F32, tag="turned", name="turned")
+            u, t = n // UNIT, n % UNIT
+            turned = turned_banks.tile([P, PACK, P], F32, tag="turned", name="turned")
+            for j in range(PACK):
                 nc.tensor.matmul(
-                    turned[:, 0, 0:WARM_COLS], lhsT=ident[:], rhs=ident[:, 0:WARM_COLS],
-                    start=True, stop=True,
+                    turned[:, j, :], lhsT=y_of[n][:, 0, j, :], rhs=ident[:],
+                    is_transpose=True, start=True, stop=False,
                 )
-                for j in range(PACK):
-                    nc.tensor.matmul(
-                        turned[:, j, :], lhsT=y_of[n][:, h, j, :], rhs=ident[:],
-                        is_transpose=True, start=True, stop=False,
-                    )
-                    if j == PACK - 1 and n >= HEAD_TILES:
-                        nc.tensor.matmul(
-                            turned[:, j, :], lhsT=offset_parts[:, h, :], rhs=ones[:],
-                            start=False, stop=True,
-                        )
-                    else:
-                        nc.tensor.matmul(
-                            turned[:, j, :], lhsT=offset_rows[:, h, j, :], rhs=ident[:],
-                            is_transpose=True, start=False, stop=True,
-                        )
-                turned_of[(n, h)] = turned
+                nc.tensor.matmul(
+                    turned[:, j, :], lhsT=offset_rows[:, j, :], rhs=ident[:],
+                    is_transpose=True, start=False, stop=True,
+                )
+            turned_of[n] = turned
+            if t == 0:
+                for i in range(2):
+                    pair = pair_banks.tile([P, 2, UNIT, P], F32, tag="pair", name="pair")
+                    pairs_of[(u, i)] = pair
+            for j in range(PACK):
+                nc.tensor.transpose(
+                    pairs_of[(u, j // 2)][:, j % 2, t, :], y_of[n][:, 1, j, :], ident[:]
+                )
 
         def gain(n):
             u, t = n // UNIT, n % UNIT
             if t == 0:
                 grouped_of[u] = work.tile(
-                    [P, UNIT, PASSES, P, PACK], BF16, tag="grouped", name="grouped",
+                    [P, PASSES, UNIT * P, PACK], BF16, tag="grouped", name="grouped",
                     align_bytes=64,
                 )
-            for h in range(PASSES):
-                nc.vector.tensor_tensor(
-                    out=grouped_of[u][:, t, h, :, :],
-                    in0=turned_of[(n, h)][:].rearrange("p j r -> p r j"),
-                    in1=gains[:, h, :].unsqueeze(1).to_broadcast([P, P, PACK]),
-                    op=ALU.mult,
+            nc.vector.tensor_tensor(
+                out=grouped_of[u][:, 0, t * P : (t + 1) * P, :],
+                in0=turned_of[n][:].rearrange("p j r -> p r j"),
+                in1=gains[:, 0, :].unsqueeze(1).to_broadcast([P, P, PACK]),
+                op=ALU.mult,
+            )
+
+
+        def scale_and_shift(u):
+            planes_of[u] = work.tile([P, PACK, UNIT * P], BF16, tag="planes", name="planes")
+            for j in range(PACK):
+                nc.scalar.activation(
+                    out=planes_of[u][:, j, :],
+                    in_=pairs_of[(u, j // 2)][:, j % 2, :, :].rearrange("p t r -> p (t r)"),
+                    func=ACT.Identity, scale=gains[:, 1, j : j + 1], bias=offsets[:, 1, j : j + 1],
                 )
 
+        def interleave(u):
+            nc.vector.tensor_copy(
+                out=grouped_of[u][:, 1, :, :].rearrange("p (w i) j -> p w j i", i=4),
+                in_=planes_of[u][:].rearrange("p j (w i) -> p w j i", i=4),
+            )
 
         def quantise(u):
-            codes = work.tile([P, UNIT, PASSES, P], U32, tag="codes", name="codes", align_bytes=64)
-            scales = work.tile([P, UNIT, PASSES, P], U8, tag="scales", name="scales", align_bytes=64)
+            codes = work.tile([P, PASSES, UNIT * P], U32, tag="codes", name="codes", align_bytes=64)
+            scales = work.tile([P, PASSES, UNIT * P], U8, tag="scales", name="scales", align_bytes=64)
             nc.vector.quantize_mx(
-                out=codes[:].rearrange("p t h r -> p (t h r)").bitcast(FP8X4),
-                scales=scales[:].rearrange("p t h r -> p (t h r)"),
-                in_=grouped_of[u][:].rearrange("p t h r j -> p (t h r j)"),
+                out=codes[:].rearrange("p h r -> p (h r)").bitcast(FP8X4),
+                scales=scales[:].rearrange("p h r -> p (h r)"),
+                in_=grouped_of[u][:].rearrange("p h r j -> p (h r j)"),
             )
             codes_of[u] = codes
             scales_of[u] = scales
@@ -175,47 +186,50 @@ def tile_transformerlayershard_pa_t_kernel(
         def project(n):
             u, t = n // UNIT, n % UNIT
             codes, scales = codes_of[u], scales_of[u]
-            qk_acc = qk_banks.tile([P, BANK], F32, tag="qk_acc", name="qk_acc")
+            rows = slice(t * P, (t + 1) * P)
             if t == 0:
+                qk_acc_of[u] = qk_banks.tile([P, UNIT, 2 * DH], F32, tag="qk_acc", name="qk_acc")
                 v_acc_of[u] = v_banks.tile([P, UNIT, DH], F32, tag="v_acc", name="v_acc")
             for acc, w_codes, w_scales in (
-                (qk_acc[:], qk_codes, qk_scales), (v_acc_of[u][:, t, :], v_codes, v_scales)
+                (qk_acc_of[u], qk_codes, qk_scales), (v_acc_of[u], v_codes, v_scales)
             ):
                 for h in range(PASSES):
                     nc.tensor.matmul_mx(
-                        out=acc,
-                        lhsT=codes[:, t, h, :].bitcast(FP8X4),
-                        lhsT_scale=scales[:, t, h, :],
+                        out=acc[:, t, :],
+                        lhsT=codes[:, h, rows].bitcast(FP8X4),
+                        lhsT_scale=scales[:, h, rows],
                         rhs=w_codes[:, h, :].bitcast(FP8X4),
                         rhs_scale=w_scales[:, h, :],
                         start=(h == 0),
                         stop=(h == PASSES - 1),
                     )
-            qk_acc_of[n] = qk_acc
 
-        def rotate(n):
-            u, t = n // UNIT, n % UNIT
-            if t == 0:
-                products_of[u] = work.tile([P, UNIT, 4, DH], F32, tag="products", name="products")
+        def rotate(u):
+            tiles = slice(u * UNIT, (u + 1) * UNIT)
+            shape = [P, UNIT, 2, 4, FREQS]
+            products = work.tile([P, UNIT, 2, 2 * DH], F32, tag="products", name="products")
             nc.vector.tensor_tensor(
-                out=products_of[u][:, t, :, :],
-                in0=qk_acc_of[n][:].rearrange("p (a w) -> p a w", a=4),
-                in1=table[:, n, :, :].rearrange("p s c -> p (s c)").unsqueeze(1)
-                .to_broadcast([P, 4, DH]),
+                out=products[:].rearrange("p t s (g c) -> p t s g c", c=FREQS),
+                in0=qk_acc_of[u][:].rearrange("p t (g c) -> p t g c", c=FREQS)
+                .unsqueeze(2).to_broadcast(shape),
+                in1=table[:, tiles, :, :].unsqueeze(3).to_broadcast(shape),
                 op=ALU.mult,
             )
+            products_of[u] = products
 
         def store_qk(u):
             tiles, products = slice(u * UNIT, (u + 1) * UNIT), products_of[u]
-            qk_out = work.tile([P, UNIT, 2, DH], F32, tag="qk_out", name="qk_out")
+            qk_out = work.tile([P, 2, UNIT, DH], F32, tag="qk_out", name="qk_out")
             nc.vector.tensor_tensor(
-                out=qk_out[:].rearrange("p t g (r c) -> p (t g r) c", r=2),
-                in0=products[:, :, :, 0:FREQS].rearrange("p t a c -> p (t a) c"),
-                in1=products[:, :, :, FREQS:DH].rearrange("p t a c -> p (t a) c"),
+                out=qk_out[:].rearrange("p g t (i e) -> p t g i e", e=2),
+                in0=products[:, :, 0, :].rearrange("p t (g i e) -> p t g i e", g=2, e=2),
+                in1=products[:, :, 1, :].rearrange("p t (g i e) -> p t g i e", g=2, e=2)[
+                    :, :, :, :, ::-1
+                ],
                 op=ALU.add,
             )
-            nc.sync.dma_start(out=q_rows[:, tiles, :], in_=qk_out[:, :, 0, :])
-            nc.sync.dma_start(out=k_rows[:, tiles, :], in_=qk_out[:, :, 1, :])
+            nc.sync.dma_start(out=q_rows[:, tiles, :], in_=qk_out[:, 0, :, :])
+            nc.sync.dma_start(out=k_rows[:, tiles, :], in_=qk_out[:, 1, :, :])
 
         def store_v(u):
             v_out = work.tile([P, UNIT, DH], F32, tag="v_out", name="v_out")
@@ -224,7 +238,7 @@ def tile_transformerlayershard_pa_t_kernel(
 
         def table_turns(g):
             shape = [P, STEP, FREQS]
-            angle_of[g] = setup.tile(shape, F32, tag="angle", name="angle", bufs=2)
+            angle_of[g] = setup.tile(shape, F32, tag="angle", name="angle", bufs=3)
             nc.vector.scalar_tensor_tensor(
                 out=angle_of[g][:], in0=turns[:].unsqueeze(1).to_broadcast(shape),
                 scalar=float(STEP * g), in1=first_angles[:], op0=ALU.mult, op1=ALU.add,
@@ -238,21 +252,31 @@ def tile_transformerlayershard_pa_t_kernel(
             )
 
         def table_parts(g):
-            parts_of[g] = setup.tile([P, STEP, FREQS], F32, tag="part", name="part", bufs=2)
-            nc.vector.tensor_tensor(
+            parts_of[g] = setup.tile([P, STEP, FREQS], F32, tag="part", name="part", bufs=3)
+            nc.gpsimd.tensor_tensor(
                 out=parts_of[g][:], in0=angle_of[g][:], in1=whole_of[g][:], op=ALU.subtract
             )
 
-        def table_values(g):
+        def table_sines(g):
             tiles, part = slice(g * STEP, (g + 1) * STEP), parts_of[g]
             nc.scalar.activation(
-                out=table[:, tiles, 1, :], in_=part[:], func=ACT.Sin, scale=2.0 * math.pi,
+                out=table[:, tiles, 1, :].rearrange("p t (i e) -> p t i e", e=2),
+                in_=part[:].rearrange("p t (i e) -> p t i e", e=2)[:, :, :, ::-1],
+                func=ACT.Sin, scale=2.0 * math.pi,
             )
-            size = setup.tile([P, STEP, FREQS], F32, tag="size", name="size", bufs=2)
-            nc.scalar.activation(out=size[:], in_=part[:], func=ACT.Abs)
             nc.scalar.activation(
-                out=table[:, tiles, 0, :], in_=size[:], func=ACT.Sin, scale=-2.0 * math.pi,
-                bias=quarter[:, 0:1],
+                out=half_sines[:, tiles, :], in_=part[:], func=ACT.Sin, scale=math.pi
+            )
+
+        def table_cosines(g):
+            tiles = slice(g * STEP, (g + 1) * STEP)
+            nc.gpsimd.tensor_tensor(
+                out=half_sines[:, tiles, :], in0=half_sines[:, tiles, :],
+                in1=half_sines[:, tiles, :], op=ALU.mult,
+            )
+            nc.gpsimd.tensor_scalar(
+                out=table[:, tiles, 0, :], in0=half_sines[:, tiles, :], scalar1=-2.0, scalar2=1.0,
+                op0=ALU.mult, op1=ALU.add,
             )
 
 
@@ -301,22 +325,18 @@ def tile_transformerlayershard_pa_t_kernel(
             )
         eps = keep.tile([P, 1], F32, name="eps")
         nc.vector.tensor_scalar(out=eps[:], in0=one[:], scalar1=EPS, scalar2=None, op0=ALU.mult)
-        quarter = keep.tile([P, 1], F32, name="quarter")
-        nc.vector.tensor_scalar(
-            out=quarter[:], in0=one[:], scalar1=math.pi / 2.0, scalar2=None, op0=ALU.mult
-        )
-        ones = keep.tile([P, P], BF16, name="ones")
-        nc.vector.memset(ones[:], 1.0)
 
         gains = keep.tile([P, PASSES, PACK], F32, name="gains")
         small = setup.tile([P, PASSES, PACK], F32, name="small")
-        ratio = setup.tile([P, PASSES, PACK], F32, name="ratio")
+        ratio = setup.tile([P, PACK], F32, name="ratio")
         first = setup.tile([P, 1], F32, name="first")
         start = setup.tile([P, FREQS], F32, name="start")
         start_whole = setup.tile([P, FREQS], F32, name="start_whole")
         first_angles = keep.tile([P, STEP, FREQS], F32, name="first_angles")
         nc.vector.tensor_copy(out=first[:], in_=first_i[:])
         nc.vector.tensor_tensor(out=small[:], in0=scale_cols[:], in1=scale_cols[:], op=ALU.mult)
+        offsets = keep.tile([P, PASSES, PACK], F32, name="offsets")
+        nc.vector.tensor_copy(out=offsets[:], in_=offset_cols[:])
         nc.vector.tensor_scalar(
             out=start[:, 0:DECADE], in0=turns_hi[:], scalar1=first[:, 0:1], scalar2=None,
             op0=ALU.mult,
@@ -337,12 +357,14 @@ def tile_transformerlayershard_pa_t_kernel(
         nc.vector.tensor_tensor(
             out=first_angles[:, 0, :], in0=start[:], in1=start_whole[:], op=ALU.subtract
         )
-        nc.vector.reciprocal(out=ratio[:], in_=gains[:])
+        nc.vector.reciprocal(out=ratio[:], in_=gains[:, 0, :])
         nc.vector.scalar_tensor_tensor(
             out=first_angles[:, 0, 0:DECADE], in0=turns_lo[:], scalar=first[:, 0:1],
             in1=first_angles[:, 0, 0:DECADE], op0=ALU.mult, op1=ALU.add,
         )
-        nc.vector.tensor_tensor(out=ratio[:], in0=ratio[:], in1=offset_cols[:], op=ALU.mult)
+        nc.vector.tensor_tensor(
+            out=ratio[:], in0=ratio[:], in1=offset_cols[:, 0, :], op=ALU.mult
+        )
 
         def more_first_angles(filled):
             nc.vector.scalar_tensor_tensor(
@@ -355,48 +377,33 @@ def tile_transformerlayershard_pa_t_kernel(
         more_first_angles(1)
         row_mean(0)
         more_first_angles(2)
-        ratio_cols = setup.tile([P, SLOTS, P], F32, name="ratio_cols")
+        ratio_cols = setup.tile([P, PACK, P], F32, name="ratio_cols")
         nc.vector.tensor_copy(
-            out=ratio_cols[:],
-            in_=ratio[:].rearrange("p h j -> p (h j)").unsqueeze(2).to_broadcast([P, SLOTS, P]),
+            out=ratio_cols[:], in_=ratio[:].unsqueeze(2).to_broadcast([P, PACK, P])
         )
         more_first_angles(4)
         row_mean(1)
-        more_first_angles(8)
         row_squares(0)
         row_squares(1)
         row_mean(2)
         table = keep.tile([P, TILES, 2, FREQS], F32, name="table")
+        half_sines = keep.tile([P, TILES, FREQS], F32, name="half_sines")
 
-        qk_grouped = setup.tile([P, PASSES, BANK, PACK], BF16, name="qk_grouped", align_bytes=64)
+        qk_grouped = setup.tile([P, PASSES, 2 * DH, PACK], BF16, name="qk_grouped", align_bytes=64)
         v_grouped = setup.tile([P, PASSES, DH, PACK], BF16, name="v_grouped", align_bytes=64)
-        qk_codes = keep.tile([P, PASSES, BANK], U32, name="qk_codes", align_bytes=64)
-        qk_scales = keep.tile([P, PASSES, BANK], U8, name="qk_scales", align_bytes=64)
+        qk_codes = keep.tile([P, PASSES, 2 * DH], U32, name="qk_codes", align_bytes=64)
+        qk_scales = keep.tile([P, PASSES, 2 * DH], U8, name="qk_scales", align_bytes=64)
         v_codes = keep.tile([P, PASSES, DH], U32, name="v_codes", align_bytes=64)
         v_scales = keep.tile([P, PASSES, DH], U8, name="v_scales", align_bytes=64)
 
         def group_weights(g):
+            out = v_grouped[:]
+            if g < 2:
+                out = qk_grouped[:, :, g * DH : (g + 1) * DH, :]
             for h in range(PASSES):
-                rows = raws[g][:, h, :, :]
-                if g == 2:
-                    nc.vector.tensor_copy(
-                        out=v_grouped[:, h, :, :], in_=rows.rearrange("p j n -> p n j")
-                    )
-                    continue
-                cols = qk_grouped[:, h, g * 2 * DH : (g + 1) * 2 * DH, :]
                 nc.vector.tensor_copy(
-                    out=cols.rearrange("p (r s c) j -> p r s c j", r=2, s=2)[:, :, 0, :, :],
-                    in_=rows.rearrange("p j (r c) -> p r c j", r=2),
+                    out=out[:, h, :, :], in_=raws[g][:, h, :, :].rearrange("p j n -> p n j")
                 )
-                for a in range(2):
-                    nc.vector.tensor_copy(
-                        out=cols.rearrange("p (r s i e) j -> p r s i e j", r=2, s=2, e=2)[
-                            :, :, 1, :, a, :
-                        ],
-                        in_=rows.rearrange("p j (r i e) -> p r i e j", r=2, e=2)[
-                            :, :, :, 1 - a, :
-                        ],
-                    )
 
         def quantise_weights():
             nc.vector.quantize_mx(
@@ -410,55 +417,24 @@ def tile_transformerlayershard_pa_t_kernel(
                 in_=v_grouped[:].rearrange("p h n j -> p (h n j)"),
             )
 
-        offset_rows = keep.tile([P, PASSES, PACK, P], F32, name="offset_rows")
-        for h in range(PASSES):
-            turned_ratio = turned_banks.tile([P, PACK, P], F32, tag="turned", name="turned_ratio")
-            for j in range(PACK):
-                nc.tensor.transpose(
-                    turned_ratio[:, j, :], ratio_cols[:, h * PACK + j, :], ident[:]
-                )
-            nc.scalar.copy(out=offset_rows[:, h, :, :], in_=turned_ratio[:])
+        offset_rows = keep.tile([P, PACK, P], F32, name="offset_rows")
+        turned_ratio = turned_banks.tile([P, PACK, P], F32, tag="turned", name="turned_ratio")
+        for j in range(PACK):
+            nc.tensor.transpose(turned_ratio[:, j, :], ratio_cols[:, j, :], ident[:])
+        nc.vector.tensor_copy(out=offset_rows[:], in_=turned_ratio[:])
 
-        offset_parts = keep.tile([P, PASSES, P], BF16, name="offset_parts")
-        rest = setup.tile([P, PASSES, P], F32, name="rest")
-        nc.gpsimd.tensor_scalar(
-            out=rest[:], in0=offset_rows[:, :, PACK - 1, :], scalar1=1.0, scalar2=0.0,
-            op0=ALU.mult, op1=ALU.add,
-        )
-        total = setup.tile([P, PASSES, P], F32, name="total")
-        for i in range(3):
-            here = setup.tile([P, 1], F32, tag="here", name="here", bufs=3)
-            nc.vector.tensor_scalar(
-                out=here[:], in0=first[:], scalar1=float(TILES * i), scalar2=None, op0=ALU.is_equal
-            )
-            part = setup.tile([P, PASSES, P], BF16, tag="offset_part", name="part", bufs=3)
-            nc.gpsimd.tensor_scalar(
-                out=part[:], in0=rest[:], scalar1=1.0, scalar2=0.0, op0=ALU.mult, op1=ALU.add
-            )
-            if i < 2:
-                nc.gpsimd.tensor_tensor(out=rest[:], in0=rest[:], in1=part[:], op=ALU.subtract)
-            chosen = total
-            if i > 0:
-                chosen = setup.tile([P, PASSES, P], F32, tag="chosen", name="chosen", bufs=2)
-            nc.gpsimd.tensor_scalar(
-                out=chosen[:], in0=part[:], scalar1=here[:, 0:1], scalar2=0.0,
-                op0=ALU.mult, op1=ALU.add,
-            )
-            if i > 0:
-                nc.gpsimd.tensor_tensor(out=total[:], in0=total[:], in1=chosen[:], op=ALU.add)
-        nc.gpsimd.tensor_scalar(
-            out=offset_parts[:], in0=total[:], scalar1=1.0, scalar2=0.0, op0=ALU.mult, op1=ALU.add
-        )
-
+        table_turns(0)
+        table_wholes(0)
         for g in range(TILES // STEP):
-            table_turns(g)
-            if g < 3:
-                group_weights(g)
-            table_wholes(g)
-            if g == 3:
-                quantise_weights()
             table_parts(g)
-            table_values(g)
+            if g + 1 < TILES // STEP:
+                table_turns(g + 1)
+                if g < 3:
+                    group_weights(g)
+                table_wholes(g + 1)
+            if g == 4:
+                quantise_weights()
+            table_sines(g)
         row_mean(3)
         row_scale(0)
         row_scale(1)
@@ -466,33 +442,40 @@ def tile_transformerlayershard_pa_t_kernel(
         normalise(0)
         turn(0)
         normalise(1)
+        table_cosines(0)
 
 
         def live(n):
             return 0 <= n < TILES
 
-        for k in range(TILES + 4):
-            u = k // UNIT
-            if k % UNIT == 0 and u + 4 < UNITS and u > 0:
+        for k in range(TILES + 6):
+            u, odd = k // UNIT, k % UNIT == 1
+            if not odd and u + 4 < UNITS and u > 0:
                 load(u + 4)
-            if live(k - 2):
-                project(k - 2)
+            if odd and live(k - 4):
+                store_v(u - 2)
+            if odd and live(k):
+                scale_and_shift(u)
+            if live(k - 3):
+                project(k - 3)
+            if not odd and live(k - 2):
+                interleave(u - 1)
             if live(k):
                 gain(k)
             if live(k + 4):
                 row_mean(k + 4)
-            if k % UNIT == 0 and u > 1:
-                store_qk(u - 2)
-            if live(k - 2):
-                rotate(k - 2)
-            if k % UNIT == 1 and live(k):
-                quantise(u)
+            if odd and live(k - 4):
+                rotate(u - 2)
+            if not odd and live(k - 2):
+                quantise(u - 1)
             if live(k + 1):
                 turn(k + 1)
             if live(k + 2):
                 row_scale(k + 2)
                 normalise(k + 2)
+            if not odd and live(k - 6):
+                store_qk(u - 3)
             if live(k + 3):
                 row_squares(k + 3)
-            if k % UNIT == 1 and live(k - 2):
-                store_v(u - 1)
+            if k % STEP == 4 and live(k + 4):
+                table_cosines((k + 4) // STEP)

@@ -30,7 +30,8 @@ ROUND_MAGIC = 12582912.0
 HI_GRID = 2.0 ** 19
 STEP = 8
 TINY = 2.0 ** -60
-HEAD_TILES = 2
+HEAD_UNITS = 4
+SHARED_MEANS = 8
 X_BUFS = 8
 
 FLOPS = 2 * S * D * 3 * DH
@@ -64,7 +65,7 @@ def tile_transformerlayershard_pa_t_kernel(
         v_banks = ctx.enter_context(tc.psum_pool(name="v_banks", bufs=1))
         ctx.enter_context(tc.manual_schedule())
 
-        x_of, neg_mean_of, squares_of, rstd_of, y_of = {}, {}, {}, {}, {}
+        x_of, neg_mean_of, squares_of, spread_of, rstd_of, y_of = {}, {}, {}, {}, {}, {}
         turned_of, pairs_of, planes_of = {}, {}, {}
         grouped_of, codes_of, scales_of = {}, {}, {}
         qk_acc_of, v_acc_of, products_of = {}, {}, {}
@@ -72,90 +73,95 @@ def tile_transformerlayershard_pa_t_kernel(
 
 
         def load(u):
-            x_u = loads.tile([P, UNIT, D], BF16, tag="x_u", name="x_u")
+            x_of[u] = loads.tile([P, UNIT, D], BF16, tag="x_u", name="x_u")
             if u == 0:
                 for t in range(UNIT):
-                    nc.sync.dma_start(out=x_u[:, t, :], in_=x_rows[:, t, :])
+                    nc.sync.dma_start(out=x_of[u][:, t, :], in_=x_rows[:, t, :])
             else:
-                nc.sync.dma_start(out=x_u[:], in_=x_rows[:, u * UNIT : (u + 1) * UNIT, :])
-            for t in range(UNIT):
-                x_of[u * UNIT + t] = x_u[:, t, :]
+                nc.sync.dma_start(out=x_of[u][:], in_=x_rows[:, u * UNIT : (u + 1) * UNIT, :])
 
-        def row_mean(n):
-            neg_mean_of[n] = stats.tile([P, 1], F32, tag="neg_mean", name="neg_mean")
-            if n < HEAD_TILES or n % 2 == 1 or n % 8 == 4:
-                unread_v = work.tile([P, D], BF16, tag="unread_v", name="unread_v")
-                nc.vector.tensor_scalar(
-                    out=unread_v[:], in0=x_of[n], scalar1=-1.0 / D, scalar2=None,
-                    op0=ALU.mult, op1=ALU.add, accum_out=neg_mean_of[n][:],
-                )
-            else:
+        def row_means(u):
+            neg_mean_of[u] = stats.tile([P, UNIT], F32, tag="neg_mean", name="neg_mean")
+            for t in range(UNIT):
+                mean = neg_mean_of[u][:, t : t + 1]
+                if t == 1 or u < HEAD_UNITS or u % SHARED_MEANS == 0:
+                    unread_v = work.tile([P, D], BF16, tag="unread_v", name="unread_v")
+                    nc.vector.tensor_scalar(
+                        out=unread_v[:], in0=x_of[u][:, t, :], scalar1=-1.0 / D, scalar2=None,
+                        op0=ALU.mult, op1=ALU.add, accum_out=mean,
+                    )
+                else:
+                    unread_s = work.tile([P, D], BF16, tag="unread_s", name="unread_s")
+                    nc.scalar.activation(
+                        out=unread_s[:], in_=x_of[u][:, t, :], func=ACT.Copy, scale=-1.0 / D,
+                        accum_out=mean,
+                    )
+
+        def row_squares(u):
+            squares_of[u] = stats.tile([P, UNIT], F32, tag="squares", name="squares")
+            for t in range(UNIT):
                 unread_s = work.tile([P, D], BF16, tag="unread_s", name="unread_s")
                 nc.scalar.activation(
-                    out=unread_s[:], in_=x_of[n], func=ACT.Copy, scale=-1.0 / D,
-                    accum_out=neg_mean_of[n][:],
+                    out=unread_s[:], in_=x_of[u][:, t, :], func=ACT.Square,
+                    bias=neg_mean_of[u][:, t : t + 1], scale=1.0,
+                    accum_out=squares_of[u][:, t : t + 1],
                 )
 
-        def row_squares(n):
-            squares_of[n] = stats.tile([P, 1], F32, tag="squares", name="squares")
-            unread_s = work.tile([P, D], BF16, tag="unread_s", name="unread_s")
+        def row_spread(u):
+            spread_of[u] = stats.tile([P, UNIT], F32, tag="spread", name="spread")
             nc.scalar.activation(
-                out=unread_s[:], in_=x_of[n], func=ACT.Square, bias=neg_mean_of[n][:, 0:1], scale=1.0,
-                accum_out=squares_of[n][:],
+                out=spread_of[u][:], in_=squares_of[u][:], func=ACT.Sqrt, scale=1.0 / D,
+                bias=eps[:, 0:1],
             )
 
-        def row_scale(n):
-            rstd_of[n] = stats.tile([P, 1], F32, tag="rstd", name="rstd")
-            nc.scalar.activation(
-                out=rstd_of[n][:], in_=squares_of[n][:], func=ACT.Abs_reciprocal_sqrt,
-                scale=1.0 / D, bias=eps[:, 0:1],
+        def row_scale(u):
+            rstd_of[u] = stats.tile([P, UNIT], F32, tag="rstd", name="rstd")
+            nc.vector.reciprocal(out=rstd_of[u][:], in_=spread_of[u][:])
+
+        def normalise(u):
+            engine = nc.vector if u == 0 or u == UNITS - 1 else nc.gpsimd
+            for t in range(UNIT):
+                y_t = work.tile([P, PASSES, PACK, P], F32, tag="y_t", name="y_t", bufs=4)
+                engine.tensor_scalar(
+                    out=y_t[:], in0=x_of[u][:, t, :].rearrange("r (h p j) -> r h j p", p=P, j=PACK),
+                    scalar1=neg_mean_of[u][:, t : t + 1], scalar2=rstd_of[u][:, t : t + 1],
+                    op0=ALU.add, op1=ALU.mult,
+                )
+                y_of[(u, t)] = y_t
+
+        def turn(u):
+            for t in range(UNIT):
+                turned = turned_banks.tile([P, PACK, P], F32, tag="turned", name="turned")
+                for j in range(PACK):
+                    nc.tensor.matmul(
+                        turned[:, j, :], lhsT=y_of[(u, t)][:, 0, j, :], rhs=ident[:],
+                        is_transpose=True, start=True, stop=False,
+                    )
+                    nc.tensor.matmul(
+                        turned[:, j, :], lhsT=offset_rows[:, j, :], rhs=ident[:],
+                        is_transpose=True, start=False, stop=True,
+                    )
+                turned_of[(u, t)] = turned
+                if t == 0:
+                    for i in range(2):
+                        pair = pair_banks.tile([P, 2, UNIT, P], F32, tag="pair", name="pair")
+                        pairs_of[(u, i)] = pair
+                for j in range(PACK):
+                    nc.tensor.transpose(
+                        pairs_of[(u, j // 2)][:, j % 2, t, :], y_of[(u, t)][:, 1, j, :], ident[:]
+                    )
+
+        def gain(u):
+            grouped_of[u] = work.tile(
+                [P, PASSES, UNIT * P, PACK], BF16, tag="grouped", name="grouped", align_bytes=64
             )
-
-        def normalise(n):
-            y_n = work.tile([P, PASSES, PACK, P], F32, tag="y_n", name="y_n")
-            engine = nc.vector if n < HEAD_TILES else nc.gpsimd
-            engine.tensor_scalar(
-                out=y_n[:], in0=x_of[n].rearrange("r (h p j) -> r h j p", p=P, j=PACK),
-                scalar1=neg_mean_of[n][:, 0:1], scalar2=rstd_of[n][:, 0:1], op0=ALU.add, op1=ALU.mult,
-            )
-            y_of[n] = y_n
-
-        def turn(n):
-            u, t = n // UNIT, n % UNIT
-            turned = turned_banks.tile([P, PACK, P], F32, tag="turned", name="turned")
-            for j in range(PACK):
-                nc.tensor.matmul(
-                    turned[:, j, :], lhsT=y_of[n][:, 0, j, :], rhs=ident[:],
-                    is_transpose=True, start=True, stop=False,
+            for t in range(UNIT):
+                nc.vector.tensor_tensor(
+                    out=grouped_of[u][:, 0, t * P : (t + 1) * P, :],
+                    in0=turned_of[(u, t)][:].rearrange("p j r -> p r j"),
+                    in1=gains[:, 0, :].unsqueeze(1).to_broadcast([P, P, PACK]),
+                    op=ALU.mult,
                 )
-                nc.tensor.matmul(
-                    turned[:, j, :], lhsT=offset_rows[:, j, :], rhs=ident[:],
-                    is_transpose=True, start=False, stop=True,
-                )
-            turned_of[n] = turned
-            if t == 0:
-                for i in range(2):
-                    pair = pair_banks.tile([P, 2, UNIT, P], F32, tag="pair", name="pair")
-                    pairs_of[(u, i)] = pair
-            for j in range(PACK):
-                nc.tensor.transpose(
-                    pairs_of[(u, j // 2)][:, j % 2, t, :], y_of[n][:, 1, j, :], ident[:]
-                )
-
-        def gain(n):
-            u, t = n // UNIT, n % UNIT
-            if t == 0:
-                grouped_of[u] = work.tile(
-                    [P, PASSES, UNIT * P, PACK], BF16, tag="grouped", name="grouped",
-                    align_bytes=64,
-                )
-            nc.vector.tensor_tensor(
-                out=grouped_of[u][:, 0, t * P : (t + 1) * P, :],
-                in0=turned_of[n][:].rearrange("p j r -> p r j"),
-                in1=gains[:, 0, :].unsqueeze(1).to_broadcast([P, P, PACK]),
-                op=ALU.mult,
-            )
-
 
         def scale_and_shift(u):
             planes_of[u] = work.tile([P, PACK, UNIT * P], BF16, tag="planes", name="planes")
@@ -183,26 +189,25 @@ def tile_transformerlayershard_pa_t_kernel(
             codes_of[u] = codes
             scales_of[u] = scales
 
-        def project(n):
-            u, t = n // UNIT, n % UNIT
+        def project(u):
             codes, scales = codes_of[u], scales_of[u]
-            rows = slice(t * P, (t + 1) * P)
-            if t == 0:
-                qk_acc_of[u] = qk_banks.tile([P, UNIT, 2 * DH], F32, tag="qk_acc", name="qk_acc")
-                v_acc_of[u] = v_banks.tile([P, UNIT, DH], F32, tag="v_acc", name="v_acc")
-            for acc, w_codes, w_scales in (
-                (qk_acc_of[u], qk_codes, qk_scales), (v_acc_of[u], v_codes, v_scales)
-            ):
-                for h in range(PASSES):
-                    nc.tensor.matmul_mx(
-                        out=acc[:, t, :],
-                        lhsT=codes[:, h, rows].bitcast(FP8X4),
-                        lhsT_scale=scales[:, h, rows],
-                        rhs=w_codes[:, h, :].bitcast(FP8X4),
-                        rhs_scale=w_scales[:, h, :],
-                        start=(h == 0),
-                        stop=(h == PASSES - 1),
-                    )
+            qk_acc = qk_banks.tile([P, UNIT, 2 * DH], F32, tag="qk_acc", name="qk_acc")
+            v_acc = v_banks.tile([P, UNIT, DH], F32, tag="v_acc", name="v_acc")
+            for acc, w_codes, w_scales in ((qk_acc, qk_codes, qk_scales), (v_acc, v_codes, v_scales)):
+                for t in range(UNIT):
+                    rows = slice(t * P, (t + 1) * P)
+                    for h in range(PASSES):
+                        nc.tensor.matmul_mx(
+                            out=acc[:, t, :],
+                            lhsT=codes[:, h, rows].bitcast(FP8X4),
+                            lhsT_scale=scales[:, h, rows],
+                            rhs=w_codes[:, h, :].bitcast(FP8X4),
+                            rhs_scale=w_scales[:, h, :],
+                            start=(h == 0),
+                            stop=(h == PASSES - 1),
+                        )
+            qk_acc_of[u] = qk_acc
+            v_acc_of[u] = v_acc
 
         def rotate(u):
             tiles = slice(u * UNIT, (u + 1) * UNIT)
@@ -245,7 +250,7 @@ def tile_transformerlayershard_pa_t_kernel(
             )
 
         def table_wholes(g):
-            whole_of[g] = setup.tile([P, STEP, FREQS], F32, tag="whole", name="whole", bufs=2)
+            whole_of[g] = setup.tile([P, STEP, FREQS], F32, tag="whole", name="whole", bufs=3)
             nc.vector.tensor_scalar(
                 out=whole_of[g][:], in0=angle_of[g][:], scalar1=ROUND_MAGIC, scalar2=ROUND_MAGIC,
                 op0=ALU.add, op1=ALU.subtract,
@@ -253,7 +258,7 @@ def tile_transformerlayershard_pa_t_kernel(
 
         def table_parts(g):
             parts_of[g] = setup.tile([P, STEP, FREQS], F32, tag="part", name="part", bufs=3)
-            nc.gpsimd.tensor_tensor(
+            nc.vector.tensor_tensor(
                 out=parts_of[g][:], in0=angle_of[g][:], in1=whole_of[g][:], op=ALU.subtract
             )
 
@@ -264,19 +269,11 @@ def tile_transformerlayershard_pa_t_kernel(
                 in_=part[:].rearrange("p t (i e) -> p t i e", e=2)[:, :, :, ::-1],
                 func=ACT.Sin, scale=2.0 * math.pi,
             )
+            size = setup.tile([P, STEP, FREQS], F32, tag="size", name="size", bufs=2)
+            nc.scalar.activation(out=size[:], in_=part[:], func=ACT.Abs)
             nc.scalar.activation(
-                out=half_sines[:, tiles, :], in_=part[:], func=ACT.Sin, scale=math.pi
-            )
-
-        def table_cosines(g):
-            tiles = slice(g * STEP, (g + 1) * STEP)
-            nc.gpsimd.tensor_tensor(
-                out=half_sines[:, tiles, :], in0=half_sines[:, tiles, :],
-                in1=half_sines[:, tiles, :], op=ALU.mult,
-            )
-            nc.gpsimd.tensor_scalar(
-                out=table[:, tiles, 0, :], in0=half_sines[:, tiles, :], scalar1=-2.0, scalar2=1.0,
-                op0=ALU.mult, op1=ALU.add,
+                out=table[:, tiles, 0, :], in_=size[:], func=ACT.Sin, scale=-2.0 * math.pi,
+                bias=quarter[:, 0:1],
             )
 
 
@@ -297,7 +294,7 @@ def tile_transformerlayershard_pa_t_kernel(
                 out=raw[:], in_=w.rearrange("(h p j) n -> p h j n", p=P, j=PACK)
             )
             raws.append(raw)
-        for u in range(2, 5):
+        for u in range(2, 6):
             load(u)
 
         ident = keep.tile([P, P], F32, name="ident")
@@ -306,6 +303,8 @@ def tile_transformerlayershard_pa_t_kernel(
         nc.gpsimd.iota(first_i[:], pattern=[[0, 1]], base=0, channel_multiplier=TILES)
         one = setup.tile([P, 1], F32, name="one")
         nc.vector.memset(one[:], 1.0)
+        unread_sine = setup.tile([P, 1], F32, name="unread_sine")
+        nc.scalar.activation(out=unread_sine[:], in_=one[:], func=ACT.Sin)
         turns_hi = setup.tile([P, DECADE], F32, name="turns_hi")
         turns_lo = setup.tile([P, DECADE], F32, name="turns_lo")
         for c in range(DECADE):
@@ -323,6 +322,10 @@ def tile_transformerlayershard_pa_t_kernel(
                 out=turns[:, d * DECADE : (d + 1) * DECADE], in0=turns[:, 0:DECADE],
                 scalar1=10.0 ** -d, scalar2=0.0, op0=ALU.mult, op1=ALU.add,
             )
+        quarter = keep.tile([P, 1], F32, name="quarter")
+        nc.vector.tensor_scalar(
+            out=quarter[:], in0=one[:], scalar1=math.pi / 2.0, scalar2=None, op0=ALU.mult
+        )
         eps = keep.tile([P, 1], F32, name="eps")
         nc.vector.tensor_scalar(out=eps[:], in0=one[:], scalar1=EPS, scalar2=None, op0=ALU.mult)
 
@@ -375,19 +378,11 @@ def tile_transformerlayershard_pa_t_kernel(
             )
 
         more_first_angles(1)
-        row_mean(0)
-        more_first_angles(2)
-        ratio_cols = setup.tile([P, PACK, P], F32, name="ratio_cols")
-        nc.vector.tensor_copy(
-            out=ratio_cols[:], in_=ratio[:].unsqueeze(2).to_broadcast([P, PACK, P])
-        )
-        more_first_angles(4)
-        row_mean(1)
+        row_means(0)
         row_squares(0)
-        row_squares(1)
-        row_mean(2)
+        more_first_angles(2)
+        more_first_angles(4)
         table = keep.tile([P, TILES, 2, FREQS], F32, name="table")
-        half_sines = keep.tile([P, TILES, FREQS], F32, name="half_sines")
 
         qk_grouped = setup.tile([P, PASSES, 2 * DH, PACK], BF16, name="qk_grouped", align_bytes=64)
         v_grouped = setup.tile([P, PASSES, DH, PACK], BF16, name="v_grouped", align_bytes=64)
@@ -417,65 +412,66 @@ def tile_transformerlayershard_pa_t_kernel(
                 in_=v_grouped[:].rearrange("p h n j -> p (h n j)"),
             )
 
+        table_turns(0)
+        table_turns(1)
+        table_wholes(0)
+        for g in range(TILES // STEP):
+            table_parts(g)
+            if g + 2 < TILES // STEP:
+                table_turns(g + 2)
+            if g + 1 < TILES // STEP:
+                table_wholes(g + 1)
+            table_sines(g)
+        ratio_cols = setup.tile([P, PACK, P], F32, name="ratio_cols")
+        nc.vector.tensor_copy(
+            out=ratio_cols[:], in_=ratio[:].unsqueeze(2).to_broadcast([P, PACK, P])
+        )
         offset_rows = keep.tile([P, PACK, P], F32, name="offset_rows")
         turned_ratio = turned_banks.tile([P, PACK, P], F32, tag="turned", name="turned_ratio")
         for j in range(PACK):
             nc.tensor.transpose(turned_ratio[:, j, :], ratio_cols[:, j, :], ident[:])
         nc.vector.tensor_copy(out=offset_rows[:], in_=turned_ratio[:])
-
-        table_turns(0)
-        table_wholes(0)
-        for g in range(TILES // STEP):
-            table_parts(g)
-            if g + 1 < TILES // STEP:
-                table_turns(g + 1)
-                if g < 3:
-                    group_weights(g)
-                table_wholes(g + 1)
-            if g == 4:
-                quantise_weights()
-            table_sines(g)
-        row_mean(3)
+        for g in range(3):
+            group_weights(g)
+        row_means(1)
+        row_spread(0)
         row_scale(0)
-        row_scale(1)
-        row_squares(2)
         normalise(0)
-        turn(0)
-        normalise(1)
-        table_cosines(0)
+        row_squares(1)
+        row_means(2)
 
 
-        def live(n):
-            return 0 <= n < TILES
+        def live(u):
+            return 0 <= u < UNITS
 
-        for k in range(TILES + 6):
-            u, odd = k // UNIT, k % UNIT == 1
-            if not odd and u + 4 < UNITS and u > 0:
-                load(u + 4)
-            if odd and live(k - 4):
-                store_v(u - 2)
-            if odd and live(k):
-                scale_and_shift(u)
-            if live(k - 3):
-                project(k - 3)
-            if not odd and live(k - 2):
-                interleave(u - 1)
-            if live(k):
-                gain(k)
-            if live(k + 4):
-                row_mean(k + 4)
-            if odd and live(k - 4):
-                rotate(u - 2)
-            if not odd and live(k - 2):
-                quantise(u - 1)
-            if live(k + 1):
-                turn(k + 1)
-            if live(k + 2):
-                row_scale(k + 2)
-                normalise(k + 2)
-            if not odd and live(k - 6):
-                store_qk(u - 3)
-            if live(k + 3):
-                row_squares(k + 3)
-            if k % STEP == 4 and live(k + 4):
-                table_cosines((k + 4) // STEP)
+        for i in range(-1, UNITS + 3):
+            if live(i + 7):
+                load(i + 7)
+            if live(i - 1):
+                store_v(i - 1)
+            if live(i + 2):
+                row_spread(i + 2)
+            if live(i):
+                interleave(i)
+            if live(i - 2):
+                store_qk(i - 2)
+            if live(i):
+                quantise(i)
+            if live(i + 2):
+                row_scale(i + 2)
+                normalise(i + 2)
+            if live(i + 1):
+                turn(i + 1)
+                gain(i + 1)
+            if i == -1:
+                quantise_weights()
+            if live(i):
+                project(i)
+            if live(i - 1):
+                rotate(i - 1)
+            if live(i + 3):
+                row_squares(i + 3)
+            if live(i + 1):
+                scale_and_shift(i + 1)
+            if live(i + 4):
+                row_means(i + 4)

import math
from contextlib import ExitStack

import concourse.mybir as mybir
from concourse.masks import make_identity

F32 = mybir.dt.float32
BF16 = mybir.dt.bfloat16
I32 = mybir.dt.int32
U32 = mybir.dt.uint32
U8 = mybir.dt.uint8
FP8X4 = mybir.dt.float8_e4m3fn_x4
ALU = mybir.AluOpType
ACT = mybir.ActivationFunctionType

P = 128
S = 8192
D = 1024
DH = 128
EPS = 1e-5
PACK = 4
PASSES = D // (P * PACK)
TILES = S // P
UNIT = 2
UNITS = TILES // UNIT
BANK = 512
FREQS = DH // 2
DECADE = FREQS // 4
ROUND_MAGIC = 12582912.0
HI_GRID = 2.0 ** 19
STEP = 8
TINY = 2.0 ** -60
HEAD_UNITS = 4
SHARED_MEANS = 8
X_BUFS = 8

FLOPS = 2 * S * D * 3 * DH


def turns_per_position(c):
    sign = -1.0 if c % 2 == 0 else 1.0
    turns = sign * 10000.0 ** (-c / FREQS) / (2.0 * math.pi)
    coarse = round(turns * HI_GRID) / HI_GRID
    return coarse, turns - coarse


def tile_transformerlayershard_pa_t_kernel(
    tc, x, ln_scale, ln_offset, Wq, Wk, Wv, out_0, out_1, out_2
):
    nc = tc.nc
    x_rows = x.rearrange("b (p t) d -> p (b t) d", t=TILES)
    q_rows = out_0.rearrange("(p t) h j -> p t (h j)", t=TILES)
    k_rows = out_1.rearrange("(p t) h j -> p t (h j)", t=TILES)
    v_rows = out_2.rearrange("(p t) h j -> p t (h j)", t=TILES)

    with ExitStack() as ctx:
        keep = ctx.enter_context(tc.tile_pool(name="keep", bufs=1))
        setup = ctx.enter_context(tc.tile_pool(name="setup", bufs=1))
        loads = ctx.enter_context(tc.tile_pool(name="loads", bufs=X_BUFS))
        stats = ctx.enter_context(tc.tile_pool(name="stats", bufs=8))
        work = ctx.enter_context(tc.tile_pool(name="work", bufs=3))
        turned_banks = ctx.enter_context(tc.psum_pool(name="turned_banks", bufs=2))
        pair_banks = ctx.enter_context(tc.psum_pool(name="pair_banks", bufs=3))
        qk_banks = ctx.enter_context(tc.psum_pool(name="qk_banks", bufs=2))
        v_banks = ctx.enter_context(tc.psum_pool(name="v_banks", bufs=1))
        ctx.enter_context(tc.manual_schedule())

        x_of, neg_mean_of, squares_of, spread_of, rstd_of, y_of = {}, {}, {}, {}, {}, {}
        turned_of, pairs_of, planes_of = {}, {}, {}
        grouped_of, codes_of, scales_of = {}, {}, {}
        qk_acc_of, v_acc_of, products_of = {}, {}, {}
        angle_of, whole_of, parts_of = {}, {}, {}


        def load(u):
            x_of[u] = loads.tile([P, UNIT, D], BF16, tag="x_u", name="x_u")
            if u == 0:
                for t in range(UNIT):
                    nc.sync.dma_start(out=x_of[u][:, t, :], in_=x_rows[:, t, :])
            else:
                nc.sync.dma_start(out=x_of[u][:], in_=x_rows[:, u * UNIT : (u + 1) * UNIT, :])

        def row_means(u):
            neg_mean_of[u] = stats.tile([P, UNIT], F32, tag="neg_mean", name="neg_mean")
            for t in range(UNIT):
                mean = neg_mean_of[u][:, t : t + 1]
                if t == 1 or u < HEAD_UNITS or u % SHARED_MEANS == 0:
                    unread_v = work.tile([P, D], BF16, tag="unread_v", name="unread_v")
                    nc.vector.tensor_scalar(
                        out=unread_v[:], in0=x_of[u][:, t, :], scalar1=-1.0 / D, scalar2=None,
                        op0=ALU.mult, op1=ALU.add, accum_out=mean,
                    )
                else:
                    unread_s = work.tile([P, D], BF16, tag="unread_s", name="unread_s")
                    nc.scalar.activation(
                        out=unread_s[:], in_=x_of[u][:, t, :], func=ACT.Copy, scale=-1.0 / D,
                        accum_out=mean,
                    )

        def row_squares(u):
            squares_of[u] = stats.tile([P, UNIT], F32, tag="squares", name="squares")
            for t in range(UNIT):
                unread_s = work.tile([P, D], BF16, tag="unread_s", name="unread_s")
                nc.scalar.activation(
                    out=unread_s[:], in_=x_of[u][:, t, :], func=ACT.Square,
                    bias=neg_mean_of[u][:, t : t + 1], scale=1.0,
                    accum_out=squares_of[u][:, t : t + 1],
                )

        def row_spread(u):
            spread_of[u] = stats.tile([P, UNIT], F32, tag="spread", name="spread")
            nc.scalar.activation(
                out=spread_of[u][:], in_=squares_of[u][:], func=ACT.Sqrt, scale=1.0 / D,
                bias=eps[:, 0:1],
            )

        def row_scale(u):
            rstd_of[u] = stats.tile([P, UNIT], F32, tag="rstd", name="rstd")
            nc.vector.reciprocal(out=rstd_of[u][:], in_=spread_of[u][:])

        def normalise(u):
            engine = nc.vector if u == 0 or u == UNITS - 1 else nc.gpsimd
            for t in range(UNIT):
                y_t = work.tile([P, PASSES, PACK, P], F32, tag="y_t", name="y_t", bufs=4)
                engine.tensor_scalar(
                    out=y_t[:], in0=x_of[u][:, t, :].rearrange("r (h p j) -> r h j p", p=P, j=PACK),
                    scalar1=neg_mean_of[u][:, t : t + 1], scalar2=rstd_of[u][:, t : t + 1],
                    op0=ALU.add, op1=ALU.mult,
                )
                y_of[(u, t)] = y_t

        def turn(u):
            for t in range(UNIT):
                turned = turned_banks.tile([P, PACK, P], F32, tag="turned", name="turned")
                for j in range(PACK):
                    nc.tensor.matmul(
                        turned[:, j, :], lhsT=y_of[(u, t)][:, 0, j, :], rhs=ident[:],
                        is_transpose=True, start=True, stop=False,
                    )
                    nc.tensor.matmul(
                        turned[:, j, :], lhsT=offset_rows[:, j, :], rhs=ident[:],
                        is_transpose=True, start=False, stop=True,
                    )
                turned_of[(u, t)] = turned
                if t == 0:
                    for i in range(2):
                        pair = pair_banks.tile([P, 2, UNIT, P], F32, tag="pair", name="pair")
                        pairs_of[(u, i)] = pair
                for j in range(PACK):
                    nc.tensor.transpose(
                        pairs_of[(u, j // 2)][:, j % 2, t, :], y_of[(u, t)][:, 1, j, :], ident[:]
                    )

        def gain(u):
            grouped_of[u] = work.tile(
                [P, PASSES, UNIT * P, PACK], BF16, tag="grouped", name="grouped", align_bytes=64
            )
            for t in range(UNIT):
                nc.vector.tensor_tensor(
                    out=grouped_of[u][:, 0, t * P : (t + 1) * P, :],
                    in0=turned_of[(u, t)][:].rearrange("p j r -> p r j"),
                    in1=gains[:, 0, :].unsqueeze(1).to_broadcast([P, P, PACK]),
                    op=ALU.mult,
                )

        def scale_and_shift(u):
            planes_of[u] = work.tile([P, PACK, UNIT * P], BF16, tag="planes", name="planes")
            for j in range(PACK):
                nc.scalar.activation(
                    out=planes_of[u][:, j, :],
                    in_=pairs_of[(u, j // 2)][:, j % 2, :, :].rearrange("p t r -> p (t r)"),
                    func=ACT.Identity, scale=gains[:, 1, j : j + 1], bias=offsets[:, 1, j : j + 1],
                )

        def interleave(u):
            nc.vector.tensor_copy(
                out=grouped_of[u][:, 1, :, :].rearrange("p (w i) j -> p w j i", i=4),
                in_=planes_of[u][:].rearrange("p j (w i) -> p w j i", i=4),
            )

        def quantise(u):
            codes = work.tile([P, PASSES, UNIT * P], U32, tag="codes", name="codes", align_bytes=64)
            scales = work.tile([P, PASSES, UNIT * P], U8, tag="scales", name="scales", align_bytes=64)
            nc.vector.quantize_mx(
                out=codes[:].rearrange("p h r -> p (h r)").bitcast(FP8X4),
                scales=scales[:].rearrange("p h r -> p (h r)"),
                in_=grouped_of[u][:].rearrange("p h r j -> p (h r j)"),
            )
            codes_of[u] = codes
            scales_of[u] = scales

        def project(u):
            codes, scales = codes_of[u], scales_of[u]
            qk_acc = qk_banks.tile([P, UNIT, 2 * DH], F32, tag="qk_acc", name="qk_acc")
            v_acc = v_banks.tile([P, UNIT, DH], F32, tag="v_acc", name="v_acc")
            for acc, w_codes, w_scales in ((qk_acc, qk_codes, qk_scales), (v_acc, v_codes, v_scales)):
                for t in range(UNIT):
                    rows = slice(t * P, (t + 1) * P)
                    for h in range(PASSES):
                        nc.tensor.matmul_mx(
                            out=acc[:, t, :],
                            lhsT=codes[:, h, rows].bitcast(FP8X4),
                            lhsT_scale=scales[:, h, rows],
                            rhs=w_codes[:, h, :].bitcast(FP8X4),
                            rhs_scale=w_scales[:, h, :],
                            start=(h == 0),
                            stop=(h == PASSES - 1),
                        )
            qk_acc_of[u] = qk_acc
            v_acc_of[u] = v_acc

        def rotate(u):
            tiles = slice(u * UNIT, (u + 1) * UNIT)
            shape = [P, UNIT, 2, 4, FREQS]
            products = work.tile([P, UNIT, 2, 2 * DH], F32, tag="products", name="products")
            nc.vector.tensor_tensor(
                out=products[:].rearrange("p t s (g c) -> p t s g c", c=FREQS),
                in0=qk_acc_of[u][:].rearrange("p t (g c) -> p t g c", c=FREQS)
                .unsqueeze(2).to_broadcast(shape),
                in1=table[:, tiles, :, :].unsqueeze(3).to_broadcast(shape),
                op=ALU.mult,
            )
            products_of[u] = products

        def store_qk(u):
            tiles, products = slice(u * UNIT, (u + 1) * UNIT), products_of[u]
            qk_out = work.tile([P, 2, UNIT, DH], F32, tag="qk_out", name="qk_out")
            nc.vector.tensor_tensor(
                out=qk_out[:].rearrange("p g t (i e) -> p t g i e", e=2),
                in0=products[:, :, 0, :].rearrange("p t (g i e) -> p t g i e", g=2, e=2),
                in1=products[:, :, 1, :].rearrange("p t (g i e) -> p t g i e", g=2, e=2)[
                    :, :, :, :, ::-1
                ],
                op=ALU.add,
            )
            nc.sync.dma_start(out=q_rows[:, tiles, :], in_=qk_out[:, 0, :, :])
            nc.sync.dma_start(out=k_rows[:, tiles, :], in_=qk_out[:, 1, :, :])

        def store_v(u):
            v_out = work.tile([P, UNIT, DH], F32, tag="v_out", name="v_out")
            nc.scalar.copy(out=v_out[:], in_=v_acc_of[u][:])
            nc.sync.dma_start(out=v_rows[:, u * UNIT : (u + 1) * UNIT, :], in_=v_out[:])

        def table_turns(g):
            shape = [P, STEP, FREQS]
            angle_of[g] = setup.tile(shape, F32, tag="angle", name="angle", bufs=3)
            nc.vector.scalar_tensor_tensor(
                out=angle_of[g][:], in0=turns[:].unsqueeze(1).to_broadcast(shape),
                scalar=float(STEP * g), in1=first_angles[:], op0=ALU.mult, op1=ALU.add,
            )

        def table_wholes(g):
            whole_of[g] = setup.tile([P, STEP, FREQS], F32, tag="whole", name="whole", bufs=3)
            nc.vector.tensor_scalar(
                out=whole_of[g][:], in0=angle_of[g][:], scalar1=ROUND_MAGIC, scalar2=ROUND_MAGIC,
                op0=ALU.add, op1=ALU.subtract,
            )

        def table_parts(g):
            parts_of[g] = setup.tile([P, STEP, FREQS], F32, tag="part", name="part", bufs=3)
            nc.vector.tensor_tensor(
                out=parts_of[g][:], in0=angle_of[g][:], in1=whole_of[g][:], op=ALU.subtract
            )

        def table_sines(g):
            tiles, part = slice(g * STEP, (g + 1) * STEP), parts_of[g]
            nc.scalar.activation(
                out=table[:, tiles, 1, :].rearrange("p t (i e) -> p t i e", e=2),
                in_=part[:].rearrange("p t (i e) -> p t i e", e=2)[:, :, :, ::-1],
                func=ACT.Sin, scale=2.0 * math.pi,
            )
            size = setup.tile([P, STEP, FREQS], F32, tag="size", name="size", bufs=2)
            nc.scalar.activation(out=size[:], in_=part[:], func=ACT.Abs)
            nc.scalar.activation(
                out=table[:, tiles, 0, :], in_=size[:], func=ACT.Sin, scale=-2.0 * math.pi,
                bias=quarter[:, 0:1],
            )


        scale_cols = setup.tile([P, PASSES, PACK], BF16, name="scale_cols")
        nc.sync.dma_start(
            out=scale_cols[:], in_=ln_scale.rearrange("(h p j) -> p h j", p=P, j=PACK)
        )
        offset_cols = setup.tile([P, PASSES, PACK], BF16, name="offset_cols")
        nc.sync.dma_start(
            out=offset_cols[:], in_=ln_offset.rearrange("(h p j) -> p h j", p=P, j=PACK)
        )
        load(0)
        load(1)
        raws = []
        for name, w in (("w_raw_q", Wq), ("w_raw_k", Wk), ("w_raw_v", Wv)):
            raw = setup.tile([P, PASSES, PACK, DH], BF16, name=name)
            nc.sync.dma_start(
                out=raw[:], in_=w.rearrange("(h p j) n -> p h j n", p=P, j=PACK)
            )
            raws.append(raw)
        for u in range(2, 6):
            load(u)

        ident = keep.tile([P, P], F32, name="ident")
        make_identity(nc, ident[:])
        first_i = setup.tile([P, 1], I32, name="first_i")
        nc.gpsimd.iota(first_i[:], pattern=[[0, 1]], base=0, channel_multiplier=TILES)
        one = setup.tile([P, 1], F32, name="one")
        nc.vector.memset(one[:], 1.0)
        unread_sine = setup.tile([P, 1], F32, name="unread_sine")
        nc.scalar.activation(out=unread_sine[:], in_=one[:], func=ACT.Sin)
        turns_hi = setup.tile([P, DECADE], F32, name="turns_hi")
        turns_lo = setup.tile([P, DECADE], F32, name="turns_lo")
        for c in range(DECADE):
            hi, lo = turns_per_position(c)
            nc.gpsimd.memset(turns_hi[:, c : c + 1], hi)
            nc.vector.tensor_scalar(
                out=turns_lo[:, c : c + 1], in0=one[:], scalar1=lo, scalar2=None, op0=ALU.mult
            )
        turns = keep.tile([P, FREQS], F32, name="turns")
        nc.gpsimd.tensor_tensor(
            out=turns[:, 0:DECADE], in0=turns_hi[:], in1=turns_lo[:], op=ALU.add
        )
        for d in range(1, FREQS // DECADE):
            nc.gpsimd.tensor_scalar(
                out=turns[:, d * DECADE : (d + 1) * DECADE], in0=turns[:, 0:DECADE],
                scalar1=10.0 ** -d, scalar2=0.0, op0=ALU.mult, op1=ALU.add,
            )
        quarter = keep.tile([P, 1], F32, name="quarter")
        nc.vector.tensor_scalar(
            out=quarter[:], in0=one[:], scalar1=math.pi / 2.0, scalar2=None, op0=ALU.mult
        )
        eps = keep.tile([P, 1], F32, name="eps")
        nc.vector.tensor_scalar(out=eps[:], in0=one[:], scalar1=EPS, scalar2=None, op0=ALU.mult)

        gains = keep.tile([P, PASSES, PACK], F32, name="gains")
        small = setup.tile([P, PASSES, PACK], F32, name="small")
        ratio = setup.tile([P, PACK], F32, name="ratio")
        first = setup.tile([P, 1], F32, name="first")
        start = setup.tile([P, FREQS], F32, name="start")
        start_whole = setup.tile([P, FREQS], F32, name="start_whole")
        first_angles = keep.tile([P, STEP, FREQS], F32, name="first_angles")
        nc.vector.tensor_copy(out=first[:], in_=first_i[:])
        nc.vector.tensor_tensor(out=small[:], in0=scale_cols[:], in1=scale_cols[:], op=ALU.mult)
        offsets = keep.tile([P, PASSES, PACK], F32, name="offsets")
        nc.vector.tensor_copy(out=offsets[:], in_=offset_cols[:])
        nc.vector.tensor_scalar(
            out=start[:, 0:DECADE], in0=turns_hi[:], scalar1=first[:, 0:1], scalar2=None,
            op0=ALU.mult,
        )
        nc.vector.tensor_scalar(
            out=start[:, DECADE:FREQS], in0=turns[:, DECADE:FREQS], scalar1=first[:, 0:1],
            scalar2=None, op0=ALU.mult,
        )
        nc.vector.tensor_scalar(
            out=small[:], in0=small[:], scalar1=TINY * TINY, scalar2=TINY,
            op0=ALU.is_lt, op1=ALU.mult,
        )
        nc.vector.tensor_scalar(
            out=start_whole[:], in0=start[:], scalar1=ROUND_MAGIC, scalar2=ROUND_MAGIC,
            op0=ALU.add, op1=ALU.subtract,
        )
        nc.vector.tensor_tensor(out=gains[:], in0=scale_cols[:], in1=small[:], op=ALU.add)
        nc.vector.tensor_tensor(
            out=first_angles[:, 0, :], in0=start[:], in1=start_whole[:], op=ALU.subtract
        )
        nc.vector.reciprocal(out=ratio[:], in_=gains[:, 0, :])
        nc.vector.scalar_tensor_tensor(
            out=first_angles[:, 0, 0:DECADE], in0=turns_lo[:], scalar=first[:, 0:1],
            in1=first_angles[:, 0, 0:DECADE], op0=ALU.mult, op1=ALU.add,
        )
        nc.vector.tensor_tensor(
            out=ratio[:], in0=ratio[:], in1=offset_cols[:, 0, :], op=ALU.mult
        )

        def more_first_angles(filled):
            nc.vector.scalar_tensor_tensor(
                out=first_angles[:, filled : 2 * filled, :],
                in0=turns[:].unsqueeze(1).to_broadcast([P, filled, FREQS]),
                scalar=float(filled), in1=first_angles[:, 0:filled, :],
                op0=ALU.mult, op1=ALU.add,
            )

        more_first_angles(1)
        row_means(0)
        row_squares(0)
        more_first_angles(2)
        more_first_angles(4)
        table = keep.tile([P, TILES, 2, FREQS], F32, name="table")

        qk_grouped = setup.tile([P, PASSES, 2 * DH, PACK], BF16, name="qk_grouped", align_bytes=64)
        v_grouped = setup.tile([P, PASSES, DH, PACK], BF16, name="v_grouped", align_bytes=64)
        qk_codes = keep.tile([P, PASSES, 2 * DH], U32, name="qk_codes", align_bytes=64)
        qk_scales = keep.tile([P, PASSES, 2 * DH], U8, name="qk_scales", align_bytes=64)
        v_codes = keep.tile([P, PASSES, DH], U32, name="v_codes", align_bytes=64)
        v_scales = keep.tile([P, PASSES, DH], U8, name="v_scales", align_bytes=64)

        def group_weights(g):
            out = v_grouped[:]
            if g < 2:
                out = qk_grouped[:, :, g * DH : (g + 1) * DH, :]
            for h in range(PASSES):
                nc.vector.tensor_copy(
                    out=out[:, h, :, :], in_=raws[g][:, h, :, :].rearrange("p j n -> p n j")
                )

        def quantise_weights():
            nc.vector.quantize_mx(
                out=qk_codes[:].rearrange("p h n -> p (h n)").bitcast(FP8X4),
                scales=qk_scales[:].rearrange("p h n -> p (h n)"),
                in_=qk_grouped[:].rearrange("p h n j -> p (h n j)"),
            )
            nc.vector.quantize_mx(
                out=v_codes[:].rearrange("p h n -> p (h n)").bitcast(FP8X4),
                scales=v_scales[:].rearrange("p h n -> p (h n)"),
                in_=v_grouped[:].rearrange("p h n j -> p (h n j)"),
            )

        table_turns(0)
        table_turns(1)
        table_wholes(0)
        for g in range(TILES // STEP):
            table_parts(g)
            if g + 2 < TILES // STEP:
                table_turns(g + 2)
            if g + 1 < TILES // STEP:
                table_wholes(g + 1)
            table_sines(g)
        ratio_cols = setup.tile([P, PACK, P], F32, name="ratio_cols")
        nc.vector.tensor_copy(
            out=ratio_cols[:], in_=ratio[:].unsqueeze(2).to_broadcast([P, PACK, P])
        )
        offset_rows = keep.tile([P, PACK, P], F32, name="offset_rows")
        turned_ratio = turned_banks.tile([P, PACK, P], F32, tag="turned", name="turned_ratio")
        for j in range(PACK):
            nc.tensor.transpose(turned_ratio[:, j, :], ratio_cols[:, j, :], ident[:])
        nc.vector.tensor_copy(out=offset_rows[:], in_=turned_ratio[:])
        for g in range(3):
            group_weights(g)
        row_means(1)
        row_spread(0)
        row_scale(0)
        normalise(0)
        row_squares(1)
        row_means(2)


        def live(u):
            return 0 <= u < UNITS

        for i in range(-1, UNITS + 3):
            if live(i + 7):
                load(i + 7)
            if live(i - 1):
                store_v(i - 1)
            if live(i + 2):
                row_spread(i + 2)
            if live(i):
                interleave(i)
            if live(i - 2):
                store_qk(i - 2)
            if live(i):
                quantise(i)
            if live(i + 2):
                row_scale(i + 2)
                normalise(i + 2)
            if live(i + 1):
                turn(i + 1)
                gain(i + 1)
            if i == -1:
                quantise_weights()
            if live(i):
                project(i)
            if live(i - 1):
                rotate(i - 1)
            if live(i + 3):
                row_squares(i + 3)
            if live(i + 1):
                scale_and_shift(i + 1)
            if live(i + 4):
                row_means(i + 4)
